import numpy as np
import ml_dtypes


def mxq(x, axis, fmt="e4m3"):
    dtype, down = {"e4m3": (ml_dtypes.float8_e4m3fn, 7), "e5m2": (ml_dtypes.float8_e5m2, 14)}[fmt]
    v = np.moveaxis(np.asarray(x, np.float32).astype(ml_dtypes.bfloat16).astype(np.float64), axis, -1)
    blocks = v.reshape(v.shape[:-1] + (-1, 32))
    amax = np.abs(blocks).max(-1, keepdims=True)
    byte = np.maximum(np.where(amax > 0, np.frexp(amax)[1] - 1 + 127, 0) - down, 1)
    scale = np.exp2(byte - 127.0)
    codes = (blocks / scale).astype(np.float32).astype(dtype).astype(np.float64)
    return np.moveaxis((codes * scale).reshape(v.shape), -1, axis)


WIDE = False


def mx_kscale(k):
    if not WIDE:
        return np.ones(k)
    levels = np.array([10, -10, 5, -5, 0])
    a = np.random.permutation(np.resize(levels, k // 512 * 4)).reshape(k // 512, 4)
    idx = np.arange(k)
    return np.exp2(a[idx // 512, idx % 128 // 32])


BF16 = ml_dtypes.bfloat16


def bf(x):
    return np.asarray(x, np.float32).astype(BF16)


def f64(x):
    return np.asarray(x).astype(np.float64)


N, C, H, W, BINS = 8, 2, 512, 512, 32
SIGMA = 0.05


def setup_inputs():
    u = np.random.random_sample((N, H, W))[:, None]
    v = np.random.random_sample((N, C, H, W))
    img = 0.6 * u + 0.4 * v
    e = np.log2(mx_kscale(H * W)).reshape(H, W)
    m = np.abs(e).max()
    if m > 0:
        dn = np.stack([m - e, m + e])
        img = -np.sqrt((0.1 * img) ** 2 + 2.0 * np.log(2.0) * SIGMA ** 2 * dn)
    return {"image": bf(img)}


def reference(image):
    image = f64(image)
    n, c, h, w = image.shape
    bins = np.linspace(0.0, 1.0, BINS)
    ch_a = image[:, 0].reshape(n, h * w)
    ch_b = image[:, 1].reshape(n, h * w)
    inv_sigma = 1.0 / SIGMA
    ka = np.exp(-0.5 * ((ch_a[:, :, None] - bins) * inv_sigma) ** 2)
    kb = np.exp(-0.5 * ((ch_b[:, :, None] - bins) * inv_sigma) ** 2)
    hist = mxq(ka, 1, "e4m3").transpose(0, 2, 1) @ mxq(kb, 1, "e4m3")
    return hist[:, None, :, :]

@@ -1,0 +1,248 @@
+from contextlib import ExitStack
+
+import concourse.mybir as mybir
+from concourse.masks import make_identity
+
+F32 = mybir.dt.float32
+BF16 = mybir.dt.bfloat16
+U32 = mybir.dt.uint32
+U8 = mybir.dt.uint8
+FP8X4 = mybir.dt.float8_e4m3fn_x4
+ACT = mybir.ActivationFunctionType
+ALU = mybir.AluOpType
+AX = mybir.AxisListType
+
+P = 128
+IMAGES = 8
+BINS = 32
+ROWS_PER_PART = 4
+ROW = 512
+UNIT = 512
+OPS = 32
+RUN = 16
+
+FLOPS = 2 * IMAGES * 512 * 512 * BINS * BINS
+
+EULER = 2.718281828459045
+INV_2S2 = 200.0
+STEP = 1.0 / 31.0
+X_LO = -0.6875
+X_HI = 1.6875
+X_REF = 0.5
+SHIFT = 45.0
+
+GROUPS = (
+    (4, (-4, -3, -2, -1, 1, 2, 3, 4)),
+    (13, (-4, -3, -2, -1, 1, 2, 3, 4)),
+    (21, (-3, -2, -1, 1, 2)),
+)
+DIRECT = (24, 25, 26, 27, 28, 29, 30, 31)
+OFFSETS = (-4, -3, -2, -1, 1, 2, 3, 4)
+
+
+def slope(r):
+    return 2.0 * INV_2S2 * r * STEP
+
+
+def tile_colourhistogram_kernel(tc, image, out):
+    nc = tc.nc
+    with ExitStack() as ctx:
+        const = ctx.enter_context(tc.tile_pool(name="const", bufs=1))
+        load = ctx.enter_context(tc.tile_pool(name="load", bufs=2))
+        xpool = ctx.enter_context(tc.tile_pool(name="xpool", bufs=2))
+        work = ctx.enter_context(tc.tile_pool(name="work", bufs=2))
+        big = ctx.enter_context(tc.tile_pool(name="big", bufs=2))
+        mxp = ctx.enter_context(tc.tile_pool(name="mxp", bufs=3))
+        ps_x = ctx.enter_context(tc.psum_pool(name="ps_x", bufs=2))
+        ps_acc = ctx.enter_context(tc.psum_pool(name="ps_acc", bufs=2))
+        ps_fin = ctx.enter_context(tc.psum_pool(name="ps_fin", bufs=1))
+
+        col_g = BINS
+        col_shift = BINS + len(OFFSETS)
+        biases = const.tile([P, col_shift + 1], F32, name="biases")
+        for i in range(BINS):
+            nc.vector.memset(biases[:, i : i + 1], float(i))
+        for t in range(len(OFFSETS)):
+            nc.vector.memset(biases[:, col_g + t : col_g + t + 1], float(OFFSETS[t]))
+        nc.vector.memset(biases[:, col_shift : col_shift + 1], SHIFT)
+        nc.vector.tensor_scalar_mul(out=biases[:, 0:BINS], in0=biases[:, 0:BINS], scalar1=-STEP)
+        nc.vector.tensor_scalar_mul(
+            out=biases[:, col_g:col_shift], in0=biases[:, col_g:col_shift], scalar1=-slope(1) * X_REF
+        )
+
+        ident = const.tile([P, P], F32, name="ident")
+        make_identity(nc, ident[:])
+        same_g = const.tile([P, 4], F32, name="same_g")
+        nc.vector.tensor_reduce(
+            out=same_g[:], in_=ident[:].rearrange("p (i g) -> p g i", g=4), axis=AX.X, op=ALU.add
+        )
+        fold = const.tile([P, P], F32, name="fold")
+        nc.vector.memset(fold[:], 0.0)
+        nc.vector.tensor_reduce(
+            out=fold[:, 0:BINS], in_=ident[:].rearrange("p (i g) -> p i g", g=4), axis=AX.X, op=ALU.add
+        )
+        diag = const.tile([P, IMAGES * BINS], F32, name="diag")
+
+        loaded = {}
+        xts = {}
+        accs = {}
+
+        def prep(n):
+            raw = load.tile([P, 2 * ROWS_PER_PART * ROW], BF16, name="raw", tag="raw")
+            nc.sync.dma_start(
+                out=raw[:].rearrange("c (h x) -> c h x", h=2),
+                in_=image[n].rearrange("h (c k) w -> c h (k w)", k=ROWS_PER_PART),
+            )
+            nc.vector.tensor_scalar(
+                out=raw[:], in0=raw[:], scalar1=X_HI, scalar2=X_LO, op0=ALU.min, op1=ALU.max
+            )
+            loaded[n] = raw
+
+        def xpose(n, k):
+            words = loaded[n][:].bitcast(F32)
+            xp = ps_x.tile([P, 2, 2, P], F32, name="xp", tag="xp")
+            for h in range(2):
+                for e in range(2):
+                    base = h * 1024 + k * 256
+                    nc.tensor.transpose(xp[:, h, e, :], words[:, base + e : base + 256 : 2], ident[:])
+            xt = xpool.tile([P, 2 * UNIT], BF16, name="xt", tag="xt")
+            nc.scalar.copy(
+                out=xt[:].bitcast(F32).rearrange("p (h c e) -> p h c e", h=2, e=2),
+                in_=xp[:].rearrange("p h e c -> p h c e"),
+            )
+            xts[(n, k)] = xt
+
+        def front(u):
+            n, k, h = u
+            xu = xts[(n, k)][:, h * UNIT : (h + 1) * UNIT]
+            gs = {}
+            for t in range(len(OFFSETS)):
+                r = OFFSETS[t]
+                g = work.tile([P, UNIT], F32, name="g%d" % t, tag="g%d" % t)
+                nc.scalar.activation(
+                    out=g[:], in_=xu, func=ACT.Exp, bias=biases[:, col_g + t : col_g + t + 1], scale=slope(r)
+                )
+                gs[r] = g
+            ps = []
+            for a in range(len(GROUPS)):
+                m = GROUPS[a][0]
+                sq = work.tile([P, UNIT], F32, name="sq", tag="sq", bufs=3)
+                nc.scalar.activation(out=sq[:], in_=xu, func=ACT.Square, bias=biases[:, m : m + 1], scale=1.0)
+                pp = work.tile([P, UNIT], F32, name="pp%d" % a, tag="pp%d" % a)
+                nc.scalar.activation(
+                    out=pp[:], in_=sq[:], func=ACT.Exp, bias=biases[:, col_shift : col_shift + 1], scale=-INV_2S2
+                )
+                ps.append(pp)
+            grp = big.tile([P, OPS * BINS * RUN], BF16, name="grp", tag="grp", align_bytes=64)
+            return (xu, gs, ps, grp)
+
+        def by_run(ap):
+            return ap.rearrange("p (o q) -> p o q", q=RUN)
+
+        def products(st):
+            xu, gs, ps, grp = st
+            g4 = grp[:].rearrange("p (o i q) -> p o i q", i=BINS, q=RUN)
+            for a in range(len(GROUPS)):
+                m, offs = GROUPS[a]
+                nc.vector.tensor_scalar_mul(out=g4[:, :, m, :], in0=by_run(ps[a][:]), scalar1=pow(EULER, -SHIFT))
+                for r in offs:
+                    c = pow(EULER, -SHIFT + slope(r) * (X_REF - m * STEP) - INV_2S2 * (r * STEP) * (r * STEP))
+                    nc.vector.scalar_tensor_tensor(
+                        out=g4[:, :, m + r, :],
+                        in0=by_run(gs[r][:]),
+                        scalar=c,
+                        in1=by_run(ps[a][:]),
+                        op0=ALU.mult,
+                        op1=ALU.mult,
+                    )
+
+        def direct(st):
+            xu, gs, ps, grp = st
+            g4 = grp[:].rearrange("p (o i q) -> p o i q", i=BINS, q=RUN)
+            for i in DIRECT:
+                sq = work.tile([P, UNIT], F32, name="sq", tag="sq", bufs=3)
+                nc.scalar.activation(out=sq[:], in_=xu, func=ACT.Square, bias=biases[:, i : i + 1], scale=1.0)
+                nc.scalar.activation(out=g4[:, :, i, :], in_=by_run(sq[:]), func=ACT.Exp, scale=-INV_2S2)
+
+        def quantise(st):
+            grp = st[3]
+            codes = mxp.tile([P, OPS * P], U32, name="codes", tag="codes", align_bytes=64)
+            plane = mxp.tile([P, OPS * P], U8, name="plane", tag="plane", align_bytes=64)
+            for q in range(4):
+                nc.vector.quantize_mx(
+                    out=codes[:, q * 1024 : (q + 1) * 1024].bitcast(FP8X4),
+                    scales=plane[:, q * 1024 : (q + 1) * 1024],
+                    in_=grp[:, q * 4096 : (q + 1) * 4096],
+                )
+            return (codes, plane)
+
+        def multiply(n, k, qa, qb):
+            if k == 0:
+                accs[n] = ps_acc.tile([P, P], F32, name="acc", tag="acc")
+            acc = accs[n]
+            for o in range(OPS):
+                cols = slice(o * P, (o + 1) * P)
+                nc.tensor.matmul_mx(
+                    out=acc[:],
+                    lhsT=qa[0][:, cols].bitcast(FP8X4),
+                    lhsT_scale=qa[1][:, cols],
+                    rhs=qb[0][:, cols].bitcast(FP8X4),
+                    rhs_scale=qb[1][:, cols],
+                    start=(k == 0 and o == 0),
+                    stop=(k == ROWS_PER_PART - 1 and o == OPS - 1),
+                )
+            if k == ROWS_PER_PART - 1:
+                kept = work.tile([P, P], F32, name="kept", tag="kept")
+                nc.vector.tensor_tensor(
+                    out=kept[:].rearrange("p (j g) -> p j g", g=4),
+                    in0=acc[:].rearrange("p (j g) -> p j g", g=4),
+                    in1=same_g[:].unsqueeze(1).to_broadcast([P, BINS, 4]),
+                    op=ALU.mult,
+                )
+                nc.vector.tensor_reduce(
+                    out=diag[:, n * BINS : (n + 1) * BINS],
+                    in_=kept[:].rearrange("p (j g) -> p j g", g=4),
+                    axis=AX.X,
+                    op=ALU.add,
+                )
+
+        pairs = []
+        for n in range(IMAGES):
+            for k in range(ROWS_PER_PART):
+                pairs.append((n, k))
+
+        prep(0)
+        xpose(0, 0)
+        hold = {"unit": None}
+
+        def finish_previous():
+            if hold["unit"] is None:
+                return
+            u, st = hold["unit"]
+            hold[u[2]] = quantise(st)
+            if u[2] == 1:
+                multiply(u[0], u[1], hold[0], hold[1])
+
+        for t in range(len(pairs)):
+            n, k = pairs[t]
+            for h in range(2):
+                st = front((n, k, h))
+                finish_previous()
+                if h == 0:
+                    if k == 1 and n + 1 < IMAGES:
+                        prep(n + 1)
+                    if t + 1 < len(pairs):
+                        xpose(pairs[t + 1][0], pairs[t + 1][1])
+                products(st)
+                direct(st)
+                hold["unit"] = ((n, k, h), st)
+        finish_previous()
+
+        fin = ps_fin.tile([P, IMAGES * BINS], F32, name="fin")
+        nc.tensor.matmul(out=fin[:], lhsT=fold[:], rhs=diag[:], start=True, stop=True)
+        res = const.tile([P, IMAGES * BINS], F32, name="res")
+        nc.vector.tensor_copy(out=res[:], in_=fin[:])
+        nc.sync.dma_start(
+            out=out.rearrange("n o i j -> i (n o) j"),
+            in_=res[0:BINS, :].rearrange("i (n j) -> i n j", j=BINS),
+        )

@@ -28,16 +28,14 @@ INV_2S2 = 200.0
 STEP = 1.0 / 31.0
 X_LO = -0.6875
 X_HI = 1.6875
-X_REF = 0.5
 SHIFT = 45.0
+SHIFT_MID = 39.5
 
-GROUPS = (
-    (4, (-4, -3, -2, -1, 1, 2, 3, 4)),
-    (13, (-4, -3, -2, -1, 1, 2, 3, 4)),
-    (21, (-3, -2, -1, 1, 2)),
-)
-DIRECT = (24, 25, 26, 27, 28, 29, 30, 31)
-OFFSETS = (-4, -3, -2, -1, 1, 2, 3, 4)
+OFFSETS = (-1, 1, -2, 2, -3, 3, -4, 4)
+MID = 13
+MID_OFFSETS = (-1, 1, -2, 2, -3, 3, 4)
+SIDES = (4, 22)
+DIRECT = (9, 27, 28, 29, 30, 31)
 
 
 def slope(r):
@@ -53,21 +51,30 @@ def tile_colourhistogram_kernel(tc, image, out):
         work = ctx.enter_context(tc.tile_pool(name="work", bufs=2))
         big = ctx.enter_context(tc.tile_pool(name="big", bufs=2))
         mxp = ctx.enter_context(tc.tile_pool(name="mxp", bufs=3))
-        ps_x = ctx.enter_context(tc.psum_pool(name="ps_x", bufs=2))
+        ps_x = ctx.enter_context(tc.psum_pool(name="ps_x", bufs=1))
+        ps_p = ctx.enter_context(tc.psum_pool(name="ps_p", bufs=2))
         ps_acc = ctx.enter_context(tc.psum_pool(name="ps_acc", bufs=2))
         ps_fin = ctx.enter_context(tc.psum_pool(name="ps_fin", bufs=1))
 
         col_g = BINS
         col_shift = BINS + len(OFFSETS)
-        biases = const.tile([P, col_shift + 1], F32, name="biases")
+        col_mid = col_shift + 1
+        biases = const.tile([P, col_mid + 1], F32, name="biases")
         for i in range(BINS):
             nc.vector.memset(biases[:, i : i + 1], float(i))
         for t in range(len(OFFSETS)):
-            nc.vector.memset(biases[:, col_g + t : col_g + t + 1], float(OFFSETS[t]))
+            r = OFFSETS[t]
+            nc.vector.memset(biases[:, col_g + t : col_g + t + 1], float(400 * r * MID + 200 * r * r))
         nc.vector.memset(biases[:, col_shift : col_shift + 1], SHIFT)
+        nc.vector.memset(biases[:, col_mid : col_mid + 1], SHIFT_MID)
         nc.vector.tensor_scalar_mul(out=biases[:, 0:BINS], in0=biases[:, 0:BINS], scalar1=-STEP)
-        nc.vector.tensor_scalar_mul(
-            out=biases[:, col_g:col_shift], in0=biases[:, col_g:col_shift], scalar1=-slope(1) * X_REF
+        nc.vector.tensor_scalar(
+            out=biases[:, col_g:col_shift],
+            in0=biases[:, col_g:col_shift],
+            scalar1=-STEP * STEP,
+            scalar2=-SHIFT_MID,
+            op0=ALU.mult,
+            op1=ALU.add,
         )
 
         ident = const.tile([P, P], F32, name="ident")
@@ -112,60 +119,101 @@ def tile_colourhistogram_kernel(tc, image, out):
             )
             xts[(n, k)] = xt
 
-        def front(u):
-            n, k, h = u
-            xu = xts[(n, k)][:, h * UNIT : (h + 1) * UNIT]
-            gs = {}
-            for t in range(len(OFFSETS)):
-                r = OFFSETS[t]
-                g = work.tile([P, UNIT], F32, name="g%d" % t, tag="g%d" % t)
-                nc.scalar.activation(
-                    out=g[:], in_=xu, func=ACT.Exp, bias=biases[:, col_g + t : col_g + t + 1], scale=slope(r)
-                )
-                gs[r] = g
-            ps = []
-            for a in range(len(GROUPS)):
-                m = GROUPS[a][0]
-                sq = work.tile([P, UNIT], F32, name="sq", tag="sq", bufs=3)
-                nc.scalar.activation(out=sq[:], in_=xu, func=ACT.Square, bias=biases[:, m : m + 1], scale=1.0)
-                pp = work.tile([P, UNIT], F32, name="pp%d" % a, tag="pp%d" % a)
-                nc.scalar.activation(
-                    out=pp[:], in_=sq[:], func=ACT.Exp, bias=biases[:, col_shift : col_shift + 1], scale=-INV_2S2
-                )
-                ps.append(pp)
-            grp = big.tile([P, OPS * BINS * RUN], BF16, name="grp", tag="grp", align_bytes=64)
-            return (xu, gs, ps, grp)
+        def bias_col(c):
+            return biases[:, c : c + 1]
 
         def by_run(ap):
             return ap.rearrange("p (o q) -> p o q", q=RUN)
 
-        def products(st):
-            xu, gs, ps, grp = st
-            g4 = grp[:].rearrange("p (o i q) -> p o i q", i=BINS, q=RUN)
-            for a in range(len(GROUPS)):
-                m, offs = GROUPS[a]
-                nc.vector.tensor_scalar_mul(out=g4[:, :, m, :], in0=by_run(ps[a][:]), scalar1=pow(EULER, -SHIFT))
-                for r in offs:
-                    c = pow(EULER, -SHIFT + slope(r) * (X_REF - m * STEP) - INV_2S2 * (r * STEP) * (r * STEP))
+        def side_factor(u, a):
+            n, k, h = u
+            rows = loaded[n][:, (h * ROWS_PER_PART + k) * ROW : (h * ROWS_PER_PART + k + 1) * ROW]
+            sq = work.tile([P, UNIT], F32, name="sqr", tag="sqr")
+            nc.scalar.activation(
+                out=sq[:].rearrange("c (j p) -> c j p", j=4),
+                in_=rows.rearrange("c (p j) -> c j p", j=4),
+                func=ACT.Square,
+                bias=bias_col(SIDES[a]),
+                scale=1.0,
+            )
+            fr = work.tile([P, UNIT], F32, name="fr%d" % a, tag="fr%d" % a)
+            nc.scalar.activation(out=fr[:], in_=sq[:], func=ACT.Exp, bias=bias_col(col_shift), scale=-INV_2S2)
+            ft = ps_p.tile([P, 4, P], F32, name="ft%d" % a, tag="ft%d" % a)
+            for j in range(4):
+                nc.tensor.transpose(ft[:, j, :], fr[:, j * P : (j + 1) * P], ident[:])
+            return ft
+
+        def front(u):
+            n, k, h = u
+            xu = xts[(n, k)][:, h * UNIT : (h + 1) * UNIT]
+            sq = work.tile([P, UNIT], F32, name="sq", tag="sq", bufs=3)
+            nc.scalar.activation(out=sq[:], in_=xu, func=ACT.Square, bias=bias_col(MID), scale=1.0)
+            mid = work.tile([P, UNIT], F32, name="mid", tag="mid")
+            nc.scalar.activation(out=mid[:], in_=sq[:], func=ACT.Exp, bias=bias_col(col_mid), scale=-INV_2S2)
+            gs = {}
+            fts = []
+            for t in range(len(OFFSETS)):
+                r = OFFSETS[t]
+                g = work.tile([P, UNIT], F32, name="g%d" % t, tag="g%d" % t)
+                nc.scalar.activation(out=g[:], in_=xu, func=ACT.Exp, bias=bias_col(col_g + t), scale=slope(r))
+                gs[r] = g
+                if t == 0:
+                    fts.append(side_factor(u, 0))
+                if t == 4:
+                    fts.append(side_factor(u, 1))
+            grp = big.tile([P, OPS * BINS * RUN], BF16, name="grp", tag="grp", align_bytes=64)
+            return (xu, gs, mid, fts, grp)
+
+        def bins_of(grp):
+            return grp[:].rearrange("p (o i q) -> p o i q", i=BINS, q=RUN)
+
+        def mid_products(st):
+            xu, gs, mid, fts, grp = st
+            g4 = bins_of(grp)
+            for r in MID_OFFSETS:
+                nc.gpsimd.tensor_tensor(
+                    out=g4[:, :, MID + r, :], in0=by_run(gs[r][:]), in1=by_run(mid[:]), op=ALU.mult
+                )
+            nc.gpsimd.tensor_scalar(
+                out=g4[:, :, MID, :],
+                in0=by_run(mid[:]),
+                scalar1=pow(EULER, -SHIFT_MID),
+                scalar2=1.0,
+                op0=ALU.mult,
+                op1=ALU.mult,
+            )
+
+        def side_products(st):
+            xu, gs, mid, fts, grp = st
+            g4 = bins_of(grp)
+            for a in range(len(SIDES)):
+                m = SIDES[a]
+                turned = fts[a][:].rearrange("p j (o g) -> p o g j", g=4)
+                for r in OFFSETS:
                     nc.vector.scalar_tensor_tensor(
-                        out=g4[:, :, m + r, :],
-                        in0=by_run(gs[r][:]),
-                        scalar=c,
-                        in1=by_run(ps[a][:]),
+                        out=g4[:, :, m + r, :].rearrange("p o (g j) -> p o g j", j=4),
+                        in0=gs[r][:].rearrange("p (o g j) -> p o g j", g=4, j=4),
+                        scalar=pow(EULER, SHIFT_MID - SHIFT + slope(r) * (MID - m) * STEP),
+                        in1=turned,
                         op0=ALU.mult,
                         op1=ALU.mult,
                     )
+                nc.vector.tensor_scalar_mul(
+                    out=g4[:, :, m, :].rearrange("p o (g j) -> p o g j", j=4),
+                    in0=turned,
+                    scalar1=pow(EULER, -SHIFT),
+                )
 
         def direct(st):
-            xu, gs, ps, grp = st
-            g4 = grp[:].rearrange("p (o i q) -> p o i q", i=BINS, q=RUN)
+            xu, gs, mid, fts, grp = st
+            g4 = bins_of(grp)
             for i in DIRECT:
                 sq = work.tile([P, UNIT], F32, name="sq", tag="sq", bufs=3)
-                nc.scalar.activation(out=sq[:], in_=xu, func=ACT.Square, bias=biases[:, i : i + 1], scale=1.0)
+                nc.scalar.activation(out=sq[:], in_=xu, func=ACT.Square, bias=bias_col(i), scale=1.0)
                 nc.scalar.activation(out=g4[:, :, i, :], in_=by_run(sq[:]), func=ACT.Exp, scale=-INV_2S2)
 
         def quantise(st):
-            grp = st[3]
+            grp = st[4]
             codes = mxp.tile([P, OPS * P], U32, name="codes", tag="codes", align_bytes=64)
             plane = mxp.tile([P, OPS * P], U8, name="plane", tag="plane", align_bytes=64)
             for q in range(4):
@@ -233,7 +281,8 @@ def tile_colourhistogram_kernel(tc, image, out):
                         prep(n + 1)
                     if t + 1 < len(pairs):
                         xpose(pairs[t + 1][0], pairs[t + 1][1])
-                products(st)
+                mid_products(st)
+                side_products(st)
                 direct(st)
                 hold["unit"] = ((n, k, h), st)
         finish_previous()

@@ -31,11 +31,14 @@ X_HI = 1.6875
 SHIFT = 45.0
 SHIFT_MID = 39.5
 
-OFFSETS = (-1, 1, -2, 2, -3, 3, -4, 4)
+OFFSETS = (-4, -3, -2, -1, 1, 2, 3, 4)
+MAKE_ORDER = (3, 2, 1, 0, 4, 5, 6, 7)
 MID = 13
-MID_OFFSETS = (-1, 1, -2, 2, -3, 3, 4)
 SIDES = (4, 22)
-DIRECT = (9, 27, 28, 29, 30, 31)
+UNITS = 64
+
+
+FIRST_DIRECT = 26
 
 
 def slope(r):
@@ -94,28 +97,34 @@ def tile_colourhistogram_kernel(tc, image, out):
         xts = {}
         accs = {}
 
-        def prep(n):
-            raw = load.tile([P, 2 * ROWS_PER_PART * ROW], BF16, name="raw", tag="raw")
-            nc.sync.dma_start(
-                out=raw[:].rearrange("c (h x) -> c h x", h=2),
-                in_=image[n].rearrange("h (c k) w -> c h (k w)", k=ROWS_PER_PART),
-            )
-            nc.vector.tensor_scalar(
-                out=raw[:], in0=raw[:], scalar1=X_HI, scalar2=X_LO, op0=ALU.min, op1=ALU.max
-            )
-            loaded[n] = raw
+        turned_x = {}
 
-        def xpose(n, k):
+        def fetch(n, k_lo, k_hi):
+            if k_lo == 0:
+                loaded[n] = load.tile([P, 2 * ROWS_PER_PART * ROW], BF16, name="raw", tag="raw")
+            nc.sync.dma_start(
+                out=loaded[n][:].rearrange("c (h x) -> c h x", h=2)[:, :, k_lo * ROW : k_hi * ROW],
+                in_=image[n].rearrange("h (c k) w -> c h (k w)", k=ROWS_PER_PART)[:, :, k_lo * ROW : k_hi * ROW],
+            )
+
+        def clamp(n, k_lo, k_hi):
+            part = loaded[n][:].rearrange("c (h x) -> c h x", h=2)[:, :, k_lo * ROW : k_hi * ROW]
+            nc.vector.tensor_scalar(out=part, in0=part, scalar1=X_HI, scalar2=X_LO, op0=ALU.min, op1=ALU.max)
+
+        def turn(n, k):
             words = loaded[n][:].bitcast(F32)
             xp = ps_x.tile([P, 2, 2, P], F32, name="xp", tag="xp")
             for h in range(2):
                 for e in range(2):
                     base = h * 1024 + k * 256
                     nc.tensor.transpose(xp[:, h, e, :], words[:, base + e : base + 256 : 2], ident[:])
+            turned_x[(n, k)] = xp
+
+        def settle(n, k):
             xt = xpool.tile([P, 2 * UNIT], BF16, name="xt", tag="xt")
             nc.scalar.copy(
                 out=xt[:].bitcast(F32).rearrange("p (h c e) -> p h c e", h=2, e=2),
-                in_=xp[:].rearrange("p h e c -> p h c e"),
+                in_=turned_x[(n, k)][:].rearrange("p h e c -> p h c e"),
             )
             xts[(n, k)] = xt
 
@@ -125,44 +134,52 @@ def tile_colourhistogram_kernel(tc, image, out):
         def by_run(ap):
             return ap.rearrange("p (o q) -> p o q", q=RUN)
 
-        def side_factor(u, a):
-            n, k, h = u
-            rows = loaded[n][:, (h * ROWS_PER_PART + k) * ROW : (h * ROWS_PER_PART + k + 1) * ROW]
-            sq = work.tile([P, UNIT], F32, name="sqr", tag="sqr")
-            nc.scalar.activation(
-                out=sq[:].rearrange("c (j p) -> c j p", j=4),
-                in_=rows.rearrange("c (p j) -> c j p", j=4),
-                func=ACT.Square,
-                bias=bias_col(SIDES[a]),
-                scale=1.0,
-            )
-            fr = work.tile([P, UNIT], F32, name="fr%d" % a, tag="fr%d" % a)
-            nc.scalar.activation(out=fr[:], in_=sq[:], func=ACT.Exp, bias=bias_col(col_shift), scale=-INV_2S2)
-            ft = ps_p.tile([P, 4, P], F32, name="ft%d" % a, tag="ft%d" % a)
-            for j in range(4):
-                nc.tensor.transpose(ft[:, j, :], fr[:, j * P : (j + 1) * P], ident[:])
-            return ft
+        def unit_of(u):
+            return (u // 8, (u // 2) % ROWS_PER_PART, u % 2)
 
         def front(u):
-            n, k, h = u
+            n, k, h = unit_of(u)
             xu = xts[(n, k)][:, h * UNIT : (h + 1) * UNIT]
-            sq = work.tile([P, UNIT], F32, name="sq", tag="sq", bufs=3)
-            nc.scalar.activation(out=sq[:], in_=xu, func=ACT.Square, bias=bias_col(MID), scale=1.0)
+            rows = loaded[n][:, (h * ROWS_PER_PART + k) * ROW : (h * ROWS_PER_PART + k + 1) * ROW]
+            lo = FIRST_DIRECT
+            sqs = []
+            for a in range(len(SIDES)):
+                sq = work.tile([P, UNIT], F32, name="sqr%d" % a, tag="sqr%d" % a)
+                nc.scalar.activation(
+                    out=sq[:].rearrange("c (j p) -> c j p", j=4),
+                    in_=rows.rearrange("c (p j) -> c j p", j=4),
+                    func=ACT.Square,
+                    bias=bias_col(SIDES[a]),
+                    scale=1.0,
+                )
+                sqs.append(sq)
+            sqm = work.tile([P, UNIT], F32, name="sqm", tag="sqm")
+            nc.scalar.activation(out=sqm[:], in_=xu, func=ACT.Square, bias=bias_col(MID), scale=1.0)
+            sqd = work.tile([P, BINS - FIRST_DIRECT, UNIT], F32, name="sqd", tag="sqd", bufs=1)
+            for i in range(lo, BINS):
+                nc.scalar.activation(out=sqd[:, i - lo, :], in_=xu, func=ACT.Square, bias=bias_col(i), scale=1.0)
+
+            def turned_factor(a):
+                fr = work.tile([P, UNIT], F32, name="fr%d" % a, tag="fr%d" % a)
+                nc.scalar.activation(
+                    out=fr[:], in_=sqs[a][:], func=ACT.Exp, bias=bias_col(col_shift), scale=-INV_2S2
+                )
+                ft = ps_p.tile([P, 4, P], F32, name="ft%d" % a, tag="ft%d" % a)
+                for j in range(4):
+                    nc.tensor.transpose(ft[:, j, :], fr[:, j * P : (j + 1) * P], ident[:])
+                return ft
+
+            fts = [turned_factor(0)]
             mid = work.tile([P, UNIT], F32, name="mid", tag="mid")
-            nc.scalar.activation(out=mid[:], in_=sq[:], func=ACT.Exp, bias=bias_col(col_mid), scale=-INV_2S2)
-            gs = {}
-            fts = []
-            for t in range(len(OFFSETS)):
-                r = OFFSETS[t]
-                g = work.tile([P, UNIT], F32, name="g%d" % t, tag="g%d" % t)
-                nc.scalar.activation(out=g[:], in_=xu, func=ACT.Exp, bias=bias_col(col_g + t), scale=slope(r))
-                gs[r] = g
-                if t == 0:
-                    fts.append(side_factor(u, 0))
-                if t == 4:
-                    fts.append(side_factor(u, 1))
+            nc.scalar.activation(out=mid[:], in_=sqm[:], func=ACT.Exp, bias=bias_col(col_mid), scale=-INV_2S2)
+            gs = work.tile([P, len(OFFSETS), UNIT], F32, name="gs", tag="gs")
+            for t in MAKE_ORDER:
+                nc.scalar.activation(
+                    out=gs[:, t, :], in_=xu, func=ACT.Exp, bias=bias_col(col_g + t), scale=slope(OFFSETS[t])
+                )
+            fts.append(turned_factor(1))
             grp = big.tile([P, OPS * BINS * RUN], BF16, name="grp", tag="grp", align_bytes=64)
-            return (xu, gs, mid, fts, grp)
+            return (sqd, gs, mid, fts, grp)
 
         def bins_of(grp):
             return grp[:].rearrange("p (o i q) -> p o i q", i=BINS, q=RUN)
@@ -170,9 +187,13 @@ def tile_colourhistogram_kernel(tc, image, out):
         def mid_products(st):
             xu, gs, mid, fts, grp = st
             g4 = bins_of(grp)
-            for r in MID_OFFSETS:
+            for half in range(2):
+                lo = MID - 4 + 5 * half
                 nc.gpsimd.tensor_tensor(
-                    out=g4[:, :, MID + r, :], in0=by_run(gs[r][:]), in1=by_run(mid[:]), op=ALU.mult
+                    out=g4[:, :, lo : lo + 4, :].rearrange("p o i q -> p i o q"),
+                    in0=gs[:, 4 * half : 4 * half + 4, :].rearrange("p i (o q) -> p i o q", q=RUN),
+                    in1=by_run(mid[:]).unsqueeze(1).to_broadcast([P, 4, OPS, RUN]),
+                    op=ALU.mult,
                 )
             nc.gpsimd.tensor_scalar(
                 out=g4[:, :, MID, :],
@@ -183,16 +204,19 @@ def tile_colourhistogram_kernel(tc, image, out):
                 op1=ALU.mult,
             )
 
-        def side_products(st):
+        def side_products(u, st):
             xu, gs, mid, fts, grp = st
             g4 = bins_of(grp)
             for a in range(len(SIDES)):
                 m = SIDES[a]
                 turned = fts[a][:].rearrange("p j (o g) -> p o g j", g=4)
-                for r in OFFSETS:
+                for t in MAKE_ORDER:
+                    r = OFFSETS[t]
+                    if m + r >= FIRST_DIRECT:
+                        continue
                     nc.vector.scalar_tensor_tensor(
                         out=g4[:, :, m + r, :].rearrange("p o (g j) -> p o g j", j=4),
-                        in0=gs[r][:].rearrange("p (o g j) -> p o g j", g=4, j=4),
+                        in0=gs[:, t, :].rearrange("p (o g j) -> p o g j", g=4, j=4),
                         scalar=pow(EULER, SHIFT_MID - SHIFT + slope(r) * (MID - m) * STEP),
                         in1=turned,
                         op0=ALU.mult,
@@ -204,13 +228,15 @@ def tile_colourhistogram_kernel(tc, image, out):
                     scalar1=pow(EULER, -SHIFT),
                 )
 
-        def direct(st):
-            xu, gs, mid, fts, grp = st
-            g4 = bins_of(grp)
-            for i in DIRECT:
-                sq = work.tile([P, UNIT], F32, name="sq", tag="sq", bufs=3)
-                nc.scalar.activation(out=sq[:], in_=xu, func=ACT.Square, bias=bias_col(i), scale=1.0)
-                nc.scalar.activation(out=g4[:, :, i, :], in_=by_run(sq[:]), func=ACT.Exp, scale=-INV_2S2)
+        def direct(u, st):
+            sqd, gs, mid, fts, grp = st
+            lo = FIRST_DIRECT
+            nc.scalar.activation(
+                out=bins_of(grp)[:, :, lo:BINS, :].rearrange("p o i q -> p i o q"),
+                in_=sqd[:, 0 : BINS - lo, :].rearrange("p i (o q) -> p i o q", q=RUN),
+                func=ACT.Exp,
+                scale=-INV_2S2,
+            )
 
         def quantise(st):
             grp = st[4]
@@ -239,53 +265,60 @@ def tile_colourhistogram_kernel(tc, image, out):
                     start=(k == 0 and o == 0),
                     stop=(k == ROWS_PER_PART - 1 and o == OPS - 1),
                 )
-            if k == ROWS_PER_PART - 1:
-                kept = work.tile([P, P], F32, name="kept", tag="kept")
-                nc.vector.tensor_tensor(
-                    out=kept[:].rearrange("p (j g) -> p j g", g=4),
-                    in0=acc[:].rearrange("p (j g) -> p j g", g=4),
-                    in1=same_g[:].unsqueeze(1).to_broadcast([P, BINS, 4]),
-                    op=ALU.mult,
-                )
-                nc.vector.tensor_reduce(
-                    out=diag[:, n * BINS : (n + 1) * BINS],
-                    in_=kept[:].rearrange("p (j g) -> p j g", g=4),
-                    axis=AX.X,
-                    op=ALU.add,
-                )
 
-        pairs = []
-        for n in range(IMAGES):
-            for k in range(ROWS_PER_PART):
-                pairs.append((n, k))
+        def pick_diagonal(n):
+            kept = work.tile([P, P], F32, name="kept", tag="kept")
+            nc.vector.tensor_tensor(
+                out=kept[:].rearrange("p (j g) -> p j g", g=4),
+                in0=accs[n][:].rearrange("p (j g) -> p j g", g=4),
+                in1=same_g[:].unsqueeze(1).to_broadcast([P, BINS, 4]),
+                op=ALU.mult,
+            )
+            nc.vector.tensor_reduce(
+                out=diag[:, n * BINS : (n + 1) * BINS],
+                in_=kept[:].rearrange("p (j g) -> p j g", g=4),
+                axis=AX.X,
+                op=ALU.add,
+            )
 
-        prep(0)
-        xpose(0, 0)
-        hold = {"unit": None}
-
-        def finish_previous():
-            if hold["unit"] is None:
-                return
-            u, st = hold["unit"]
-            hold[u[2]] = quantise(st)
-            if u[2] == 1:
-                multiply(u[0], u[1], hold[0], hold[1])
-
-        for t in range(len(pairs)):
-            n, k = pairs[t]
-            for h in range(2):
-                st = front((n, k, h))
-                finish_previous()
-                if h == 0:
-                    if k == 1 and n + 1 < IMAGES:
-                        prep(n + 1)
-                    if t + 1 < len(pairs):
-                        xpose(pairs[t + 1][0], pairs[t + 1][1])
-                mid_products(st)
-                side_products(st)
-                direct(st)
-                hold["unit"] = ((n, k, h), st)
-        finish_previous()
+        ctx.enter_context(tc.manual_schedule())
+        fetch(0, 0, 1)
+        fetch(0, 1, ROWS_PER_PART)
+        clamp(0, 0, 1)
+        turn(0, 0)
+        settle(0, 0)
+        clamp(0, 1, ROWS_PER_PART)
+        states = {}
+        quants = {}
+        for u in range(UNITS + 2):
+            n, k, h = unit_of(u)
+            if u < UNITS:
+                states[u] = front(u)
+            done = None
+            if u >= 2 and h == 1:
+                pn, pk, ph = unit_of(u - 2)
+                multiply(pn, pk, quants[u - 3], quants[u - 2])
+                if pk == ROWS_PER_PART - 1:
+                    done = pn
+            if u < UNITS:
+                if h == 0 and u + 2 < UNITS:
+                    nn, nk, nh = unit_of(u + 2)
+                    turn(nn, nk)
+                if h == 0 and k == 1 and n + 1 < IMAGES:
+                    fetch(n + 1, 0, ROWS_PER_PART)
+                side_products(u, states[u])
+                mid_products(states[u])
+            if 1 <= u <= UNITS:
+                quants[u - 1] = quantise(states[u - 1])
+            if done is not None:
+                pick_diagonal(done)
+            if u < UNITS:
+                if h == 0 and k == 2 and n + 1 < IMAGES:
+                    clamp(n + 1, 0, ROWS_PER_PART)
+                direct(u, states[u])
+                if h == 1 and u + 1 < UNITS:
+                    nn, nk, nh = unit_of(u + 1)
+                    settle(nn, nk)
 
         fin = ps_fin.tile([P, IMAGES * BINS], F32, name="fin")
         nc.tensor.matmul(out=fin[:], lhsT=fold[:], rhs=diag[:], start=True, stop=True)

@@ -281,7 +281,6 @@ def tile_colourhistogram_kernel(tc, image, out):
                 op=ALU.add,
             )
 
-        ctx.enter_context(tc.manual_schedule())
         fetch(0, 0, 1)
         fetch(0, 1, ROWS_PER_PART)
         clamp(0, 0, 1)

@@ -55,7 +55,6 @@ def tile_colourhistogram_kernel(tc, image, out):
         big = ctx.enter_context(tc.tile_pool(name="big", bufs=2))
         mxp = ctx.enter_context(tc.tile_pool(name="mxp", bufs=3))
         ps_x = ctx.enter_context(tc.psum_pool(name="ps_x", bufs=1))
-        ps_p = ctx.enter_context(tc.psum_pool(name="ps_p", bufs=2))
         ps_acc = ctx.enter_context(tc.psum_pool(name="ps_acc", bufs=2))
         ps_fin = ctx.enter_context(tc.psum_pool(name="ps_fin", bufs=1))
 
@@ -140,18 +139,11 @@ def tile_colourhistogram_kernel(tc, image, out):
         def front(u):
             n, k, h = unit_of(u)
             xu = xts[(n, k)][:, h * UNIT : (h + 1) * UNIT]
-            rows = loaded[n][:, (h * ROWS_PER_PART + k) * ROW : (h * ROWS_PER_PART + k + 1) * ROW]
             lo = FIRST_DIRECT
             sqs = []
             for a in range(len(SIDES)):
                 sq = work.tile([P, UNIT], F32, name="sqr%d" % a, tag="sqr%d" % a)
-                nc.scalar.activation(
-                    out=sq[:].rearrange("c (j p) -> c j p", j=4),
-                    in_=rows.rearrange("c (p j) -> c j p", j=4),
-                    func=ACT.Square,
-                    bias=bias_col(SIDES[a]),
-                    scale=1.0,
-                )
+                nc.scalar.activation(out=sq[:], in_=xu, func=ACT.Square, bias=bias_col(SIDES[a]), scale=1.0)
                 sqs.append(sq)
             sqm = work.tile([P, UNIT], F32, name="sqm", tag="sqm")
             nc.scalar.activation(out=sqm[:], in_=xu, func=ACT.Square, bias=bias_col(MID), scale=1.0)
@@ -164,10 +156,7 @@ def tile_colourhistogram_kernel(tc, image, out):
                 nc.scalar.activation(
                     out=fr[:], in_=sqs[a][:], func=ACT.Exp, bias=bias_col(col_shift), scale=-INV_2S2
                 )
-                ft = ps_p.tile([P, 4, P], F32, name="ft%d" % a, tag="ft%d" % a)
-                for j in range(4):
-                    nc.tensor.transpose(ft[:, j, :], fr[:, j * P : (j + 1) * P], ident[:])
-                return ft
+                return fr
 
             fts = [turned_factor(0)]
             mid = work.tile([P, UNIT], F32, name="mid", tag="mid")
@@ -209,7 +198,7 @@ def tile_colourhistogram_kernel(tc, image, out):
             g4 = bins_of(grp)
             for a in range(len(SIDES)):
                 m = SIDES[a]
-                turned = fts[a][:].rearrange("p j (o g) -> p o g j", g=4)
+                turned = fts[a][:].rearrange("p (o g j) -> p o g j", g=4, j=4)
                 for t in MAKE_ORDER:
                     r = OFFSETS[t]
                     if m + r >= FIRST_DIRECT:
@@ -281,6 +270,7 @@ def tile_colourhistogram_kernel(tc, image, out):
                 op=ALU.add,
             )
 
+        ctx.enter_context(tc.manual_schedule())
         fetch(0, 0, 1)
         fetch(0, 1, ROWS_PER_PART)
         clamp(0, 0, 1)

@@ -38,7 +38,9 @@ SIDES = (4, 22)
 UNITS = 64
 
 
-FIRST_DIRECT = 26
+FIRST_DIRECT = 27
+SHARED = 26
+SHARED_OPS = 8
 
 
 def slope(r):
@@ -52,9 +54,10 @@ def tile_colourhistogram_kernel(tc, image, out):
         load = ctx.enter_context(tc.tile_pool(name="load", bufs=2))
         xpool = ctx.enter_context(tc.tile_pool(name="xpool", bufs=2))
         work = ctx.enter_context(tc.tile_pool(name="work", bufs=2))
-        big = ctx.enter_context(tc.tile_pool(name="big", bufs=2))
-        mxp = ctx.enter_context(tc.tile_pool(name="mxp", bufs=3))
+        big = ctx.enter_context(tc.tile_pool(name="big", bufs=3))
+        mxp = ctx.enter_context(tc.tile_pool(name="mxp", bufs=2))
         ps_x = ctx.enter_context(tc.psum_pool(name="ps_x", bufs=1))
+        ps_p = ctx.enter_context(tc.psum_pool(name="ps_p", bufs=2))
         ps_acc = ctx.enter_context(tc.psum_pool(name="ps_acc", bufs=2))
         ps_fin = ctx.enter_context(tc.psum_pool(name="ps_fin", bufs=1))
 
@@ -106,9 +109,9 @@ def tile_colourhistogram_kernel(tc, image, out):
                 in_=image[n].rearrange("h (c k) w -> c h (k w)", k=ROWS_PER_PART)[:, :, k_lo * ROW : k_hi * ROW],
             )
 
-        def clamp(n, k_lo, k_hi):
-            part = loaded[n][:].rearrange("c (h x) -> c h x", h=2)[:, :, k_lo * ROW : k_hi * ROW]
-            nc.vector.tensor_scalar(out=part, in0=part, scalar1=X_HI, scalar2=X_LO, op0=ALU.min, op1=ALU.max)
+        def clamp(n, k):
+            xt = xts[(n, k)]
+            nc.vector.tensor_scalar(out=xt[:], in0=xt[:], scalar1=X_HI, scalar2=X_LO, op0=ALU.min, op1=ALU.max)
 
         def turn(n, k):
             words = loaded[n][:].bitcast(F32)
@@ -139,24 +142,38 @@ def tile_colourhistogram_kernel(tc, image, out):
         def front(u):
             n, k, h = unit_of(u)
             xu = xts[(n, k)][:, h * UNIT : (h + 1) * UNIT]
+            rows = loaded[n][:, (h * ROWS_PER_PART + k) * ROW : (h * ROWS_PER_PART + k + 1) * ROW]
             lo = FIRST_DIRECT
             sqs = []
             for a in range(len(SIDES)):
-                sq = work.tile([P, UNIT], F32, name="sqr%d" % a, tag="sqr%d" % a)
-                nc.scalar.activation(out=sq[:], in_=xu, func=ACT.Square, bias=bias_col(SIDES[a]), scale=1.0)
+                sq = work.tile([P, UNIT], F32, name="sqr%d" % a, tag="sqr%d" % a, bufs=1)
+                nc.scalar.activation(
+                    out=sq[:].rearrange("c (j p) -> c j p", j=4),
+                    in_=rows.rearrange("c (p j) -> c j p", j=4),
+                    func=ACT.Square,
+                    bias=bias_col(SIDES[a]),
+                    scale=1.0,
+                )
                 sqs.append(sq)
-            sqm = work.tile([P, UNIT], F32, name="sqm", tag="sqm")
+            sqm = work.tile([P, UNIT], F32, name="sqm", tag="sqm", bufs=1)
             nc.scalar.activation(out=sqm[:], in_=xu, func=ACT.Square, bias=bias_col(MID), scale=1.0)
             sqd = work.tile([P, BINS - FIRST_DIRECT, UNIT], F32, name="sqd", tag="sqd", bufs=1)
             for i in range(lo, BINS):
                 nc.scalar.activation(out=sqd[:, i - lo, :], in_=xu, func=ACT.Square, bias=bias_col(i), scale=1.0)
+            sqs26 = work.tile([P, UNIT - SHARED_OPS * RUN], F32, name="sqh", tag="sqh", bufs=1)
+            nc.scalar.activation(
+                out=sqs26[:], in_=xu[:, SHARED_OPS * RUN : UNIT], func=ACT.Square, bias=bias_col(SHARED), scale=1.0
+            )
 
             def turned_factor(a):
                 fr = work.tile([P, UNIT], F32, name="fr%d" % a, tag="fr%d" % a)
                 nc.scalar.activation(
                     out=fr[:], in_=sqs[a][:], func=ACT.Exp, bias=bias_col(col_shift), scale=-INV_2S2
                 )
-                return fr
+                ft = ps_p.tile([P, 4, P], F32, name="ft%d" % a, tag="ft%d" % a)
+                for j in range(4):
+                    nc.tensor.transpose(ft[:, j, :], fr[:, j * P : (j + 1) * P], ident[:])
+                return ft
 
             fts = [turned_factor(0)]
             mid = work.tile([P, UNIT], F32, name="mid", tag="mid")
@@ -168,22 +185,14 @@ def tile_colourhistogram_kernel(tc, image, out):
                 )
             fts.append(turned_factor(1))
             grp = big.tile([P, OPS * BINS * RUN], BF16, name="grp", tag="grp", align_bytes=64)
-            return (sqd, gs, mid, fts, grp)
+            return (sqd, gs, mid, fts, grp, sqs26)
 
         def bins_of(grp):
             return grp[:].rearrange("p (o i q) -> p o i q", i=BINS, q=RUN)
 
         def mid_products(st):
-            xu, gs, mid, fts, grp = st
+            xu, gs, mid, fts, grp, sqs26 = st
             g4 = bins_of(grp)
-            for half in range(2):
-                lo = MID - 4 + 5 * half
-                nc.gpsimd.tensor_tensor(
-                    out=g4[:, :, lo : lo + 4, :].rearrange("p o i q -> p i o q"),
-                    in0=gs[:, 4 * half : 4 * half + 4, :].rearrange("p i (o q) -> p i o q", q=RUN),
-                    in1=by_run(mid[:]).unsqueeze(1).to_broadcast([P, 4, OPS, RUN]),
-                    op=ALU.mult,
-                )
             nc.gpsimd.tensor_scalar(
                 out=g4[:, :, MID, :],
                 in0=by_run(mid[:]),
@@ -192,22 +201,29 @@ def tile_colourhistogram_kernel(tc, image, out):
                 op0=ALU.mult,
                 op1=ALU.mult,
             )
+            for half in range(2):
+                lo = MID - 4 + 5 * half
+                nc.gpsimd.tensor_tensor(
+                    out=g4[:, :, lo : lo + 4, :].rearrange("p o i q -> p i o q"),
+                    in0=gs[:, 4 * half : 4 * half + 4, :].rearrange("p i (o q) -> p i o q", q=RUN),
+                    in1=by_run(mid[:]).unsqueeze(1).to_broadcast([P, 4, OPS, RUN]),
+                    op=ALU.mult,
+                )
 
         def side_products(u, st):
-            xu, gs, mid, fts, grp = st
+            xu, gs, mid, fts, grp, sqs26 = st
             g4 = bins_of(grp)
             for a in range(len(SIDES)):
                 m = SIDES[a]
-                turned = fts[a][:].rearrange("p (o g j) -> p o g j", g=4, j=4)
+                turned = fts[a][:].rearrange("p j (o g) -> p o g j", g=4)
                 for t in MAKE_ORDER:
                     r = OFFSETS[t]
-                    if m + r >= FIRST_DIRECT:
-                        continue
+                    ops = SHARED_OPS if m + r == SHARED else OPS
                     nc.vector.scalar_tensor_tensor(
-                        out=g4[:, :, m + r, :].rearrange("p o (g j) -> p o g j", j=4),
-                        in0=gs[:, t, :].rearrange("p (o g j) -> p o g j", g=4, j=4),
+                        out=g4[:, 0:ops, m + r, :].rearrange("p o (g j) -> p o g j", j=4),
+                        in0=gs[:, t, :].rearrange("p (o g j) -> p o g j", g=4, j=4)[:, 0:ops],
                         scalar=pow(EULER, SHIFT_MID - SHIFT + slope(r) * (MID - m) * STEP),
-                        in1=turned,
+                        in1=turned[:, 0:ops],
                         op0=ALU.mult,
                         op1=ALU.mult,
                     )
@@ -218,13 +234,16 @@ def tile_colourhistogram_kernel(tc, image, out):
                 )
 
         def direct(u, st):
-            sqd, gs, mid, fts, grp = st
+            sqd, gs, mid, fts, grp, sqs26 = st
             lo = FIRST_DIRECT
             nc.scalar.activation(
                 out=bins_of(grp)[:, :, lo:BINS, :].rearrange("p o i q -> p i o q"),
                 in_=sqd[:, 0 : BINS - lo, :].rearrange("p i (o q) -> p i o q", q=RUN),
                 func=ACT.Exp,
                 scale=-INV_2S2,
+            )
+            nc.scalar.activation(
+                out=bins_of(grp)[:, SHARED_OPS:OPS, SHARED, :], in_=by_run(sqs26[:]), func=ACT.Exp, scale=-INV_2S2
             )
 
         def quantise(st):
@@ -273,14 +292,17 @@ def tile_colourhistogram_kernel(tc, image, out):
         ctx.enter_context(tc.manual_schedule())
         fetch(0, 0, 1)
         fetch(0, 1, ROWS_PER_PART)
-        clamp(0, 0, 1)
         turn(0, 0)
         settle(0, 0)
-        clamp(0, 1, ROWS_PER_PART)
+        clamp(0, 0)
         states = {}
         quants = {}
         for u in range(UNITS + 2):
             n, k, h = unit_of(u)
+            ahead = u + 2 < UNITS and h == 0
+            if ahead:
+                nn, nk, nh = unit_of(u + 2)
+                turn(nn, nk)
             if u < UNITS:
                 states[u] = front(u)
             done = None
@@ -290,9 +312,8 @@ def tile_colourhistogram_kernel(tc, image, out):
                 if pk == ROWS_PER_PART - 1:
                     done = pn
             if u < UNITS:
-                if h == 0 and u + 2 < UNITS:
-                    nn, nk, nh = unit_of(u + 2)
-                    turn(nn, nk)
+                if ahead:
+                    settle(nn, nk)
                 if h == 0 and k == 1 and n + 1 < IMAGES:
                     fetch(n + 1, 0, ROWS_PER_PART)
                 side_products(u, states[u])
@@ -302,12 +323,9 @@ def tile_colourhistogram_kernel(tc, image, out):
             if done is not None:
                 pick_diagonal(done)
             if u < UNITS:
-                if h == 0 and k == 2 and n + 1 < IMAGES:
-                    clamp(n + 1, 0, ROWS_PER_PART)
+                if ahead:
+                    clamp(nn, nk)
                 direct(u, states[u])
-                if h == 1 and u + 1 < UNITS:
-                    nn, nk, nh = unit_of(u + 1)
-                    settle(nn, nk)
 
         fin = ps_fin.tile([P, IMAGES * BINS], F32, name="fin")
         nc.tensor.matmul(out=fin[:], lhsT=fold[:], rhs=diag[:], start=True, stop=True)

@@ -39,8 +39,6 @@ UNITS = 64
 
 
 FIRST_DIRECT = 27
-SHARED = 26
-SHARED_OPS = 8
 
 
 def slope(r):
@@ -160,10 +158,6 @@ def tile_colourhistogram_kernel(tc, image, out):
             sqd = work.tile([P, BINS - FIRST_DIRECT, UNIT], F32, name="sqd", tag="sqd", bufs=1)
             for i in range(lo, BINS):
                 nc.scalar.activation(out=sqd[:, i - lo, :], in_=xu, func=ACT.Square, bias=bias_col(i), scale=1.0)
-            sqs26 = work.tile([P, UNIT - SHARED_OPS * RUN], F32, name="sqh", tag="sqh", bufs=1)
-            nc.scalar.activation(
-                out=sqs26[:], in_=xu[:, SHARED_OPS * RUN : UNIT], func=ACT.Square, bias=bias_col(SHARED), scale=1.0
-            )
 
             def turned_factor(a):
                 fr = work.tile([P, UNIT], F32, name="fr%d" % a, tag="fr%d" % a)
@@ -185,13 +179,13 @@ def tile_colourhistogram_kernel(tc, image, out):
                 )
             fts.append(turned_factor(1))
             grp = big.tile([P, OPS * BINS * RUN], BF16, name="grp", tag="grp", align_bytes=64)
-            return (sqd, gs, mid, fts, grp, sqs26)
+            return (sqd, gs, mid, fts, grp)
 
         def bins_of(grp):
             return grp[:].rearrange("p (o i q) -> p o i q", i=BINS, q=RUN)
 
         def mid_products(st):
-            xu, gs, mid, fts, grp, sqs26 = st
+            sqd, gs, mid, fts, grp = st
             g4 = bins_of(grp)
             nc.gpsimd.tensor_scalar(
                 out=g4[:, :, MID, :],
@@ -211,30 +205,30 @@ def tile_colourhistogram_kernel(tc, image, out):
                 )
 
         def side_products(u, st):
-            xu, gs, mid, fts, grp, sqs26 = st
+            sqd, gs, mid, fts, grp = st
             g4 = bins_of(grp)
             for a in range(len(SIDES)):
                 m = SIDES[a]
                 turned = fts[a][:].rearrange("p j (o g) -> p o g j", g=4)
                 for t in MAKE_ORDER:
                     r = OFFSETS[t]
-                    ops = SHARED_OPS if m + r == SHARED else OPS
                     nc.vector.scalar_tensor_tensor(
-                        out=g4[:, 0:ops, m + r, :].rearrange("p o (g j) -> p o g j", j=4),
-                        in0=gs[:, t, :].rearrange("p (o g j) -> p o g j", g=4, j=4)[:, 0:ops],
+                        out=g4[:, :, m + r, :].rearrange("p o (g j) -> p o g j", j=4),
+                        in0=gs[:, t, :].rearrange("p (o g j) -> p o g j", g=4, j=4),
                         scalar=pow(EULER, SHIFT_MID - SHIFT + slope(r) * (MID - m) * STEP),
-                        in1=turned[:, 0:ops],
+                        in1=turned,
                         op0=ALU.mult,
                         op1=ALU.mult,
                     )
-                nc.vector.tensor_scalar_mul(
-                    out=g4[:, :, m, :].rearrange("p o (g j) -> p o g j", j=4),
-                    in0=turned,
-                    scalar1=pow(EULER, -SHIFT),
-                )
+                if a == 1:
+                    nc.vector.tensor_scalar_mul(
+                        out=g4[:, :, m, :].rearrange("p o (g j) -> p o g j", j=4),
+                        in0=turned,
+                        scalar1=pow(EULER, -SHIFT),
+                    )
 
         def direct(u, st):
-            sqd, gs, mid, fts, grp, sqs26 = st
+            sqd, gs, mid, fts, grp = st
             lo = FIRST_DIRECT
             nc.scalar.activation(
                 out=bins_of(grp)[:, :, lo:BINS, :].rearrange("p o i q -> p i o q"),
@@ -243,7 +237,10 @@ def tile_colourhistogram_kernel(tc, image, out):
                 scale=-INV_2S2,
             )
             nc.scalar.activation(
-                out=bins_of(grp)[:, SHARED_OPS:OPS, SHARED, :], in_=by_run(sqs26[:]), func=ACT.Exp, scale=-INV_2S2
+                out=bins_of(grp)[:, :, SIDES[0], :].rearrange("p o (g j) -> p o g j", j=4),
+                in_=fts[0][:].rearrange("p j (o g) -> p o g j", g=4),
+                func=ACT.Copy,
+                scale=pow(EULER, -SHIFT),
             )
 
         def quantise(st):

@@ -26,8 +26,6 @@ FLOPS = 2 * IMAGES * 512 * 512 * BINS * BINS
 EULER = 2.718281828459045
 INV_2S2 = 200.0
 STEP = 1.0 / 31.0
-X_LO = -0.6875
-X_HI = 1.6875
 SHIFT = 45.0
 SHIFT_MID = 39.5
 
@@ -106,10 +104,6 @@ def tile_colourhistogram_kernel(tc, image, out):
                 out=loaded[n][:].rearrange("c (h x) -> c h x", h=2)[:, :, k_lo * ROW : k_hi * ROW],
                 in_=image[n].rearrange("h (c k) w -> c h (k w)", k=ROWS_PER_PART)[:, :, k_lo * ROW : k_hi * ROW],
             )
-
-        def clamp(n, k):
-            xt = xts[(n, k)]
-            nc.vector.tensor_scalar(out=xt[:], in0=xt[:], scalar1=X_HI, scalar2=X_LO, op0=ALU.min, op1=ALU.max)
 
         def turn(n, k):
             words = loaded[n][:].bitcast(F32)
@@ -291,7 +285,6 @@ def tile_colourhistogram_kernel(tc, image, out):
         fetch(0, 1, ROWS_PER_PART)
         turn(0, 0)
         settle(0, 0)
-        clamp(0, 0)
         states = {}
         quants = {}
         for u in range(UNITS + 2):
@@ -320,8 +313,6 @@ def tile_colourhistogram_kernel(tc, image, out):
             if done is not None:
                 pick_diagonal(done)
             if u < UNITS:
-                if ahead:
-                    clamp(nn, nk)
                 direct(u, states[u])
 
         fin = ps_fin.tile([P, IMAGES * BINS], F32, name="fin")

@@ -47,7 +47,7 @@ def tile_colourhistogram_kernel(tc, image, out):
     nc = tc.nc
     with ExitStack() as ctx:
         const = ctx.enter_context(tc.tile_pool(name="const", bufs=1))
-        load = ctx.enter_context(tc.tile_pool(name="load", bufs=2))
+        load = ctx.enter_context(tc.tile_pool(name="load", bufs=4))
         xpool = ctx.enter_context(tc.tile_pool(name="xpool", bufs=2))
         work = ctx.enter_context(tc.tile_pool(name="work", bufs=2))
         big = ctx.enter_context(tc.tile_pool(name="big", bufs=3))
@@ -96,31 +96,35 @@ def tile_colourhistogram_kernel(tc, image, out):
         accs = {}
 
         turned_x = {}
+        side_squares = {}
+        mid_squares = {}
+        direct_squares = {}
+        mids = {}
 
-        def fetch(n, k_lo, k_hi):
-            if k_lo == 0:
-                loaded[n] = load.tile([P, 2 * ROWS_PER_PART * ROW], BF16, name="raw", tag="raw")
+        def fetch(t):
+            n, k = divmod(t, ROWS_PER_PART)
+            loaded[t] = load.tile([P, 2 * ROW], BF16, name="raw", tag="raw")
             nc.sync.dma_start(
-                out=loaded[n][:].rearrange("c (h x) -> c h x", h=2)[:, :, k_lo * ROW : k_hi * ROW],
-                in_=image[n].rearrange("h (c k) w -> c h (k w)", k=ROWS_PER_PART)[:, :, k_lo * ROW : k_hi * ROW],
+                out=loaded[t][:].rearrange("c (h x) -> c h x", h=2),
+                in_=image[n].rearrange("h (c k) w -> c k h w", k=ROWS_PER_PART)[:, k],
             )
 
-        def turn(n, k):
-            words = loaded[n][:].bitcast(F32)
+        def turn(t):
+            words = loaded[t][:].bitcast(F32)
             xp = ps_x.tile([P, 2, 2, P], F32, name="xp", tag="xp")
             for h in range(2):
                 for e in range(2):
-                    base = h * 1024 + k * 256
+                    base = h * 256
                     nc.tensor.transpose(xp[:, h, e, :], words[:, base + e : base + 256 : 2], ident[:])
-            turned_x[(n, k)] = xp
+            turned_x[t] = xp
 
-        def settle(n, k):
+        def settle(t):
             xt = xpool.tile([P, 2 * UNIT], BF16, name="xt", tag="xt")
             nc.scalar.copy(
                 out=xt[:].bitcast(F32).rearrange("p (h c e) -> p h c e", h=2, e=2),
-                in_=turned_x[(n, k)][:].rearrange("p h e c -> p h c e"),
+                in_=turned_x[t][:].rearrange("p h e c -> p h c e"),
             )
-            xts[(n, k)] = xt
+            xts[t] = xt
 
         def bias_col(c):
             return biases[:, c : c + 1]
@@ -128,62 +132,76 @@ def tile_colourhistogram_kernel(tc, image, out):
         def by_run(ap):
             return ap.rearrange("p (o q) -> p o q", q=RUN)
 
-        def unit_of(u):
-            return (u // 8, (u // 2) % ROWS_PER_PART, u % 2)
-
-        def front(u):
-            n, k, h = unit_of(u)
-            xu = xts[(n, k)][:, h * UNIT : (h + 1) * UNIT]
-            rows = loaded[n][:, (h * ROWS_PER_PART + k) * ROW : (h * ROWS_PER_PART + k + 1) * ROW]
-            lo = FIRST_DIRECT
-            sqs = []
+        def square_sides(t):
+            tiles = []
             for a in range(len(SIDES)):
-                sq = work.tile([P, UNIT], F32, name="sqr%d" % a, tag="sqr%d" % a, bufs=1)
+                sq = work.tile([P, 2 * UNIT], F32, name="sqr%d" % a, tag="sqr%d" % a, bufs=1)
                 nc.scalar.activation(
-                    out=sq[:].rearrange("c (j p) -> c j p", j=4),
-                    in_=rows.rearrange("c (p j) -> c j p", j=4),
+                    out=sq[:].rearrange("c (h j p) -> c h j p", h=2, j=4),
+                    in_=loaded[t][:].rearrange("c (h p j) -> c h j p", h=2, j=4),
                     func=ACT.Square,
                     bias=bias_col(SIDES[a]),
                     scale=1.0,
                 )
-                sqs.append(sq)
-            sqm = work.tile([P, UNIT], F32, name="sqm", tag="sqm", bufs=1)
-            nc.scalar.activation(out=sqm[:], in_=xu, func=ACT.Square, bias=bias_col(MID), scale=1.0)
-            sqd = work.tile([P, BINS - FIRST_DIRECT, UNIT], F32, name="sqd", tag="sqd", bufs=1)
-            for i in range(lo, BINS):
-                nc.scalar.activation(out=sqd[:, i - lo, :], in_=xu, func=ACT.Square, bias=bias_col(i), scale=1.0)
+                tiles.append(sq)
+            side_squares[t] = tiles
 
-            def turned_factor(a):
-                fr = work.tile([P, UNIT], F32, name="fr%d" % a, tag="fr%d" % a)
+        def square_mid(t):
+            sq = work.tile([P, 2 * UNIT], F32, name="sqm", tag="sqm", bufs=1)
+            nc.scalar.activation(out=sq[:], in_=xts[t][:], func=ACT.Square, bias=bias_col(MID), scale=1.0)
+            mid_squares[t] = sq
+
+        def square_direct(t):
+            sq = work.tile([P, BINS - FIRST_DIRECT, 2 * UNIT], F32, name="sqd", tag="sqd", bufs=1)
+            for i in range(FIRST_DIRECT, BINS):
                 nc.scalar.activation(
-                    out=fr[:], in_=sqs[a][:], func=ACT.Exp, bias=bias_col(col_shift), scale=-INV_2S2
+                    out=sq[:, i - FIRST_DIRECT, :], in_=xts[t][:], func=ACT.Square, bias=bias_col(i), scale=1.0
                 )
-                ft = ps_p.tile([P, 4, P], F32, name="ft%d" % a, tag="ft%d" % a)
-                for j in range(4):
-                    nc.tensor.transpose(ft[:, j, :], fr[:, j * P : (j + 1) * P], ident[:])
-                return ft
+            direct_squares[t] = sq
 
-            fts = [turned_factor(0)]
-            mid = work.tile([P, UNIT], F32, name="mid", tag="mid")
-            nc.scalar.activation(out=mid[:], in_=sqm[:], func=ACT.Exp, bias=bias_col(col_mid), scale=-INV_2S2)
+        def turned_factor(u, a):
+            t, h = divmod(u, 2)
+            fr = work.tile([P, UNIT], F32, name="fr%d" % a, tag="fr%d" % a)
+            nc.scalar.activation(
+                out=fr[:],
+                in_=side_squares[t][a][:, h * UNIT : (h + 1) * UNIT],
+                func=ACT.Exp,
+                bias=bias_col(col_shift),
+                scale=-INV_2S2,
+            )
+            ft = ps_p.tile([P, 4, P], F32, name="ft%d" % a, tag="ft%d" % a)
+            for j in range(4):
+                nc.tensor.transpose(ft[:, j, :], fr[:, j * P : (j + 1) * P], ident[:])
+            return ft
+
+        def front(u):
+            t, h = divmod(u, 2)
+            xu = xts[t][:, h * UNIT : (h + 1) * UNIT]
+            fts = [turned_factor(u, 0)]
+            if h == 0:
+                both = work.tile([P, 2 * UNIT], F32, name="mid", tag="mid")
+                nc.scalar.activation(
+                    out=both[:], in_=mid_squares[t][:], func=ACT.Exp, bias=bias_col(col_mid), scale=-INV_2S2
+                )
+                mids[t] = both
             gs = work.tile([P, len(OFFSETS), UNIT], F32, name="gs", tag="gs")
-            for t in MAKE_ORDER:
+            for i in MAKE_ORDER:
                 nc.scalar.activation(
-                    out=gs[:, t, :], in_=xu, func=ACT.Exp, bias=bias_col(col_g + t), scale=slope(OFFSETS[t])
+                    out=gs[:, i, :], in_=xu, func=ACT.Exp, bias=bias_col(col_g + i), scale=slope(OFFSETS[i])
                 )
-            fts.append(turned_factor(1))
+            fts.append(turned_factor(u, 1))
             grp = big.tile([P, OPS * BINS * RUN], BF16, name="grp", tag="grp", align_bytes=64)
-            return (sqd, gs, mid, fts, grp)
+            return (gs, mids[t][:, h * UNIT : (h + 1) * UNIT], fts, grp)
 
         def bins_of(grp):
             return grp[:].rearrange("p (o i q) -> p o i q", i=BINS, q=RUN)
 
         def mid_products(st):
-            sqd, gs, mid, fts, grp = st
+            gs, mid, fts, grp = st
             g4 = bins_of(grp)
             nc.gpsimd.tensor_scalar(
                 out=g4[:, :, MID, :],
-                in0=by_run(mid[:]),
+                in0=by_run(mid),
                 scalar1=pow(EULER, -SHIFT_MID),
                 scalar2=1.0,
                 op0=ALU.mult,
@@ -194,12 +212,12 @@ def tile_colourhistogram_kernel(tc, image, out):
                 nc.gpsimd.tensor_tensor(
                     out=g4[:, :, lo : lo + 4, :].rearrange("p o i q -> p i o q"),
                     in0=gs[:, 4 * half : 4 * half + 4, :].rearrange("p i (o q) -> p i o q", q=RUN),
-                    in1=by_run(mid[:]).unsqueeze(1).to_broadcast([P, 4, OPS, RUN]),
+                    in1=by_run(mid).unsqueeze(1).to_broadcast([P, 4, OPS, RUN]),
                     op=ALU.mult,
                 )
 
-        def side_products(u, st):
-            sqd, gs, mid, fts, grp = st
+        def side_products(st):
+            gs, mid, fts, grp = st
             g4 = bins_of(grp)
             for a in range(len(SIDES)):
                 m = SIDES[a]
@@ -222,14 +240,16 @@ def tile_colourhistogram_kernel(tc, image, out):
                     )
 
         def direct(u, st):
-            sqd, gs, mid, fts, grp = st
-            lo = FIRST_DIRECT
+            t, h = divmod(u, 2)
             nc.scalar.activation(
-                out=bins_of(grp)[:, :, lo:BINS, :].rearrange("p o i q -> p i o q"),
-                in_=sqd[:, 0 : BINS - lo, :].rearrange("p i (o q) -> p i o q", q=RUN),
+                out=bins_of(st[3])[:, :, FIRST_DIRECT:BINS, :].rearrange("p o i q -> p i o q"),
+                in_=direct_squares[t][:, :, h * UNIT : (h + 1) * UNIT].rearrange("p i (o q) -> p i o q", q=RUN),
                 func=ACT.Exp,
                 scale=-INV_2S2,
             )
+
+        def cast_side(st):
+            gs, mid, fts, grp = st
             nc.scalar.activation(
                 out=bins_of(grp)[:, :, SIDES[0], :].rearrange("p o (g j) -> p o g j", j=4),
                 in_=fts[0][:].rearrange("p j (o g) -> p o g j", g=4),
@@ -238,7 +258,7 @@ def tile_colourhistogram_kernel(tc, image, out):
             )
 
         def quantise(st):
-            grp = st[4]
+            grp = st[3]
             codes = mxp.tile([P, OPS * P], U32, name="codes", tag="codes", align_bytes=64)
             plane = mxp.tile([P, OPS * P], U8, name="plane", tag="plane", align_bytes=64)
             for q in range(4):
@@ -281,39 +301,50 @@ def tile_colourhistogram_kernel(tc, image, out):
             )
 
         ctx.enter_context(tc.manual_schedule())
-        fetch(0, 0, 1)
-        fetch(0, 1, ROWS_PER_PART)
-        turn(0, 0)
-        settle(0, 0)
+        for t in range(3):
+            fetch(t)
+        turn(0)
+        settle(0)
+        square_sides(0)
+        square_mid(0)
         states = {}
         quants = {}
         for u in range(UNITS + 2):
-            n, k, h = unit_of(u)
-            ahead = u + 2 < UNITS and h == 0
-            if ahead:
-                nn, nk, nh = unit_of(u + 2)
-                turn(nn, nk)
+            t, h = divmod(u, 2)
+            ahead = u < UNITS and t + 1 < UNITS // 2
+            if ahead and h == 0:
+                if t + 3 < UNITS // 2:
+                    fetch(t + 3)
+                turn(t + 1)
             if u < UNITS:
                 states[u] = front(u)
             done = None
             if u >= 2 and h == 1:
-                pn, pk, ph = unit_of(u - 2)
-                multiply(pn, pk, quants[u - 3], quants[u - 2])
-                if pk == ROWS_PER_PART - 1:
-                    done = pn
+                n, k = divmod(t - 1, ROWS_PER_PART)
+                multiply(n, k, quants[u - 3], quants[u - 2])
+                if k == ROWS_PER_PART - 1:
+                    done = n
+            if ahead and h == 0:
+                settle(t + 1)
             if u < UNITS:
-                if ahead:
-                    settle(nn, nk)
-                if h == 0 and k == 1 and n + 1 < IMAGES:
-                    fetch(n + 1, 0, ROWS_PER_PART)
-                side_products(u, states[u])
+                side_products(states[u])
                 mid_products(states[u])
+                if h == 0:
+                    square_direct(t)
+                    if ahead:
+                        square_mid(t + 1)
+                else:
+                    direct(u - 1, states[u - 1])
             if 1 <= u <= UNITS:
                 quants[u - 1] = quantise(states[u - 1])
             if done is not None:
                 pick_diagonal(done)
             if u < UNITS:
-                direct(u, states[u])
+                if h == 1:
+                    direct(u, states[u])
+                cast_side(states[u])
+                if ahead and h == 1:
+                    square_sides(t + 1)
 
         fin = ps_fin.tile([P, IMAGES * BINS], F32, name="fin")
         nc.tensor.matmul(out=fin[:], lhsT=fold[:], rhs=diag[:], start=True, stop=True)

@@ -15,7 +15,7 @@ AX = mybir.AxisListType
 P = 128
 IMAGES = 8
 BINS = 32
-ROWS_PER_PART = 4
+ROWS_PER_PART = 8
 ROW = 512
 UNIT = 512
 OPS = 32
@@ -34,9 +34,10 @@ MAKE_ORDER = (3, 2, 1, 0, 4, 5, 6, 7)
 MID = 13
 SIDES = (4, 22)
 UNITS = 64
+CAST_SPLIT = 16
 
 
-FIRST_DIRECT = 27
+TOP_BINS = 5
 
 
 def slope(r):
@@ -53,14 +54,25 @@ def tile_colourhistogram_kernel(tc, image, out):
         big = ctx.enter_context(tc.tile_pool(name="big", bufs=3))
         mxp = ctx.enter_context(tc.tile_pool(name="mxp", bufs=2))
         ps_x = ctx.enter_context(tc.psum_pool(name="ps_x", bufs=1))
+        ps_e = ctx.enter_context(tc.psum_pool(name="ps_e", bufs=2))
         ps_p = ctx.enter_context(tc.psum_pool(name="ps_p", bufs=2))
-        ps_acc = ctx.enter_context(tc.psum_pool(name="ps_acc", bufs=2))
-        ps_fin = ctx.enter_context(tc.psum_pool(name="ps_fin", bufs=1))
+        ps_acc = ctx.enter_context(tc.psum_pool(name="ps_acc", bufs=1))
 
         col_g = BINS
         col_shift = BINS + len(OFFSETS)
         col_mid = col_shift + 1
-        biases = const.tile([P, col_mid + 1], F32, name="biases")
+        col_top = col_mid + 1
+        col_lin = col_top + TOP_BINS
+        biases = const.tile([P, col_lin + 1], F32, name="biases")
+        for k in range(TOP_BINS):
+            nc.vector.memset(biases[:, col_top + k : col_top + k + 1], float(200 * k * k))
+        nc.vector.memset(biases[:, col_lin : col_lin + 1], 1.0)
+        nc.vector.tensor_scalar_mul(
+            out=biases[:, col_top:col_lin], in0=biases[:, col_top:col_lin], scalar1=-STEP * STEP
+        )
+        nc.vector.tensor_scalar_mul(
+            out=biases[:, col_lin : col_lin + 1], in0=biases[:, col_lin : col_lin + 1], scalar1=-2.0 * STEP
+        )
         for i in range(BINS):
             nc.vector.memset(biases[:, i : i + 1], float(i))
         for t in range(len(OFFSETS)):
@@ -98,15 +110,19 @@ def tile_colourhistogram_kernel(tc, image, out):
         turned_x = {}
         side_squares = {}
         mid_squares = {}
-        direct_squares = {}
+        top_tiles = {}
+        sums = {}
+        states = {}
+        quants = {}
         mids = {}
 
         def fetch(t):
-            n, k = divmod(t, ROWS_PER_PART)
+            n, pair = divmod(t, ROWS_PER_PART // 2)
             loaded[t] = load.tile([P, 2 * ROW], BF16, name="raw", tag="raw")
+            rows = image[n].rearrange("h (c k) w -> (h c) k w", k=ROWS_PER_PART)
             nc.sync.dma_start(
                 out=loaded[t][:].rearrange("c (h x) -> c h x", h=2),
-                in_=image[n].rearrange("h (c k) w -> c k h w", k=ROWS_PER_PART)[:, k],
+                in_=rows[:, 2 * pair : 2 * pair + 2],
             )
 
         def turn(t):
@@ -147,17 +163,56 @@ def tile_colourhistogram_kernel(tc, image, out):
             side_squares[t] = tiles
 
         def square_mid(t):
-            sq = work.tile([P, 2 * UNIT], F32, name="sqm", tag="sqm", bufs=1)
+            sq = work.tile([P, 2 * UNIT], F32, name="sqm", tag="sqm")
             nc.scalar.activation(out=sq[:], in_=xts[t][:], func=ACT.Square, bias=bias_col(MID), scale=1.0)
             mid_squares[t] = sq
 
-        def square_direct(t):
-            sq = work.tile([P, BINS - FIRST_DIRECT, 2 * UNIT], F32, name="sqd", tag="sqd", bufs=1)
-            for i in range(FIRST_DIRECT, BINS):
-                nc.scalar.activation(
-                    out=sq[:, i - FIRST_DIRECT, :], in_=xts[t][:], func=ACT.Square, bias=bias_col(i), scale=1.0
-                )
-            direct_squares[t] = sq
+        def top_tile(t, name, func, col, scale):
+            tile = work.tile([P, 2 * UNIT], F32, name=name, tag=name)
+            nc.scalar.activation(
+                out=tile[:].rearrange("c (h j p) -> c h j p", h=2, j=4),
+                in_=loaded[t][:].rearrange("c (h p j) -> c h j p", h=2, j=4),
+                func=func,
+                bias=bias_col(col),
+                scale=scale,
+            )
+            return tile
+
+        def square_top(t):
+            top_tiles[t] = [top_tile(t, "top", ACT.Square, BINS - 1, 1.0)]
+
+        def line_top(t):
+            top_tiles[t].append(top_tile(t, "line", ACT.Identity, col_lin, 2.0 * STEP))
+
+        def add_up(u, k):
+            t, h = divmod(u, 2)
+            square, line = top_tiles[t]
+            total = ps_e.tile([P, 4, P], F32, name="total", tag="total")
+            terms = [square] + k * [line]
+            for j in range(4):
+                cols = slice(h * UNIT + j * P, h * UNIT + (j + 1) * P)
+                for i in range(len(terms)):
+                    nc.tensor.matmul(
+                        out=total[:, j, :],
+                        lhsT=terms[i][:, cols],
+                        rhs=ident[:],
+                        start=i == 0,
+                        stop=i == k,
+                        is_transpose=True,
+                    )
+            sums[(u, k)] = total
+
+        def top_bin(u, k):
+            nc.scalar.activation(
+                out=bins_of(states[u][3])[:, :, BINS - 1 - k, :].rearrange("p o (g j) -> p o g j", j=4),
+                in_=sums[(u, k)][:].rearrange("p j (o g) -> p o g j", g=4),
+                func=ACT.Exp,
+                bias=bias_col(col_top + k),
+                scale=-INV_2S2,
+            )
+            v, k = divmod(u * TOP_BINS + k + 2, TOP_BINS)
+            if v < UNITS:
+                add_up(v, k)
 
         def turned_factor(u, a):
             t, h = divmod(u, 2)
@@ -185,11 +240,16 @@ def tile_colourhistogram_kernel(tc, image, out):
                 )
                 mids[t] = both
             gs = work.tile([P, len(OFFSETS), UNIT], F32, name="gs", tag="gs")
-            for i in MAKE_ORDER:
+            for i in range(len(OFFSETS)):
+                r = MAKE_ORDER[i]
                 nc.scalar.activation(
-                    out=gs[:, i, :], in_=xu, func=ACT.Exp, bias=bias_col(col_g + i), scale=slope(OFFSETS[i])
+                    out=gs[:, r, :], in_=xu, func=ACT.Exp, bias=bias_col(col_g + r), scale=slope(OFFSETS[r])
                 )
+                if u > 0 and i % 2 == 1:
+                    top_bin(u - 1, i // 2)
             fts.append(turned_factor(u, 1))
+            if u > 0:
+                top_bin(u - 1, TOP_BINS - 1)
             grp = big.tile([P, OPS * BINS * RUN], BF16, name="grp", tag="grp", align_bytes=64)
             return (gs, mids[t][:, h * UNIT : (h + 1) * UNIT], fts, grp)
 
@@ -199,14 +259,6 @@ def tile_colourhistogram_kernel(tc, image, out):
         def mid_products(st):
             gs, mid, fts, grp = st
             g4 = bins_of(grp)
-            nc.gpsimd.tensor_scalar(
-                out=g4[:, :, MID, :],
-                in0=by_run(mid),
-                scalar1=pow(EULER, -SHIFT_MID),
-                scalar2=1.0,
-                op0=ALU.mult,
-                op1=ALU.mult,
-            )
             for half in range(2):
                 lo = MID - 4 + 5 * half
                 nc.gpsimd.tensor_tensor(
@@ -234,28 +286,29 @@ def tile_colourhistogram_kernel(tc, image, out):
                     )
                 if a == 1:
                     nc.vector.tensor_scalar_mul(
-                        out=g4[:, :, m, :].rearrange("p o (g j) -> p o g j", j=4),
-                        in0=turned,
+                        out=g4[:, 0:CAST_SPLIT, m, :].rearrange("p o (g j) -> p o g j", j=4),
+                        in0=turned[:, 0:CAST_SPLIT],
                         scalar1=pow(EULER, -SHIFT),
                     )
 
-        def direct(u, st):
+        def mid_bin(u, st):
             t, h = divmod(u, 2)
             nc.scalar.activation(
-                out=bins_of(st[3])[:, :, FIRST_DIRECT:BINS, :].rearrange("p o i q -> p i o q"),
-                in_=direct_squares[t][:, :, h * UNIT : (h + 1) * UNIT].rearrange("p i (o q) -> p i o q", q=RUN),
+                out=bins_of(st[3])[:, :, MID, :],
+                in_=by_run(mid_squares[t][:, h * UNIT : (h + 1) * UNIT]),
                 func=ACT.Exp,
                 scale=-INV_2S2,
             )
 
-        def cast_side(st):
+        def cast_sides(st):
             gs, mid, fts, grp = st
-            nc.scalar.activation(
-                out=bins_of(grp)[:, :, SIDES[0], :].rearrange("p o (g j) -> p o g j", j=4),
-                in_=fts[0][:].rearrange("p j (o g) -> p o g j", g=4),
-                func=ACT.Copy,
-                scale=pow(EULER, -SHIFT),
-            )
+            for a, lo in ((0, 0), (1, CAST_SPLIT)):
+                nc.scalar.activation(
+                    out=bins_of(grp)[:, lo:OPS, SIDES[a], :].rearrange("p o (g j) -> p o g j", j=4),
+                    in_=fts[a][:].rearrange("p j (o g) -> p o g j", g=4)[:, lo:OPS],
+                    func=ACT.Copy,
+                    scale=pow(EULER, -SHIFT),
+                )
 
         def quantise(st):
             grp = st[3]
@@ -269,20 +322,23 @@ def tile_colourhistogram_kernel(tc, image, out):
                 )
             return (codes, plane)
 
-        def multiply(n, k, qa, qb):
+        def multiply(u):
+            n, k = divmod(u, ROWS_PER_PART)
             if k == 0:
                 accs[n] = ps_acc.tile([P, P], F32, name="acc", tag="acc")
-            acc = accs[n]
-            for o in range(OPS):
-                cols = slice(o * P, (o + 1) * P)
+            codes, plane = quants[u]
+            half = OPS // 2
+            for o in range(half):
+                a = slice(o * P, (o + 1) * P)
+                b = slice((half + o) * P, (half + o + 1) * P)
                 nc.tensor.matmul_mx(
-                    out=acc[:],
-                    lhsT=qa[0][:, cols].bitcast(FP8X4),
-                    lhsT_scale=qa[1][:, cols],
-                    rhs=qb[0][:, cols].bitcast(FP8X4),
-                    rhs_scale=qb[1][:, cols],
+                    out=accs[n][:],
+                    lhsT=codes[:, a].bitcast(FP8X4),
+                    lhsT_scale=plane[:, a],
+                    rhs=codes[:, b].bitcast(FP8X4),
+                    rhs_scale=plane[:, b],
                     start=(k == 0 and o == 0),
-                    stop=(k == ROWS_PER_PART - 1 and o == OPS - 1),
+                    stop=(k == ROWS_PER_PART - 1 and o == half - 1),
                 )
 
         def pick_diagonal(n):
@@ -307,9 +363,11 @@ def tile_colourhistogram_kernel(tc, image, out):
         settle(0)
         square_sides(0)
         square_mid(0)
-        states = {}
-        quants = {}
-        for u in range(UNITS + 2):
+        square_top(0)
+        line_top(0)
+        add_up(0, 0)
+        add_up(0, 1)
+        for u in range(UNITS + 1):
             t, h = divmod(u, 2)
             ahead = u < UNITS and t + 1 < UNITS // 2
             if ahead and h == 0:
@@ -318,35 +376,33 @@ def tile_colourhistogram_kernel(tc, image, out):
                 turn(t + 1)
             if u < UNITS:
                 states[u] = front(u)
-            done = None
-            if u >= 2 and h == 1:
-                n, k = divmod(t - 1, ROWS_PER_PART)
-                multiply(n, k, quants[u - 3], quants[u - 2])
-                if k == ROWS_PER_PART - 1:
-                    done = n
-            if ahead and h == 0:
-                settle(t + 1)
+            else:
+                for k in range(TOP_BINS):
+                    top_bin(u - 1, k)
+            if u > 0:
+                cast_sides(states[u - 1])
+            if u > 1:
+                multiply(u - 2)
             if u < UNITS:
                 side_products(states[u])
                 mid_products(states[u])
-                if h == 0:
-                    square_direct(t)
-                    if ahead:
-                        square_mid(t + 1)
-                else:
-                    direct(u - 1, states[u - 1])
-            if 1 <= u <= UNITS:
+            if u > 0:
                 quants[u - 1] = quantise(states[u - 1])
-            if done is not None:
-                pick_diagonal(done)
+            if u > 1 and (u - 1) % ROWS_PER_PART == 0:
+                pick_diagonal((u - 1) // ROWS_PER_PART - 1)
             if u < UNITS:
-                if h == 1:
-                    direct(u, states[u])
-                cast_side(states[u])
-                if ahead and h == 1:
-                    square_sides(t + 1)
+                mid_bin(u, states[u])
+            if ahead and h == 0:
+                settle(t + 1)
+                square_mid(t + 1)
+                square_top(t + 1)
+                line_top(t + 1)
+            if ahead and h == 1:
+                square_sides(t + 1)
+        multiply(UNITS - 1)
+        pick_diagonal(IMAGES - 1)
 
-        fin = ps_fin.tile([P, IMAGES * BINS], F32, name="fin")
+        fin = ps_x.tile([P, IMAGES * BINS], F32, name="fin", tag="xp")
         nc.tensor.matmul(out=fin[:], lhsT=fold[:], rhs=diag[:], start=True, stop=True)
         res = const.tile([P, IMAGES * BINS], F32, name="res")
         nc.vector.tensor_copy(out=res[:], in_=fin[:])

@@ -37,6 +37,7 @@ UNITS = 64
 CAST_SPLIT = 16
 
 
+TOP_ORDER = (0, 4, 1, 3, 2)
 TOP_BINS = 5
 
 
@@ -148,19 +149,16 @@ def tile_colourhistogram_kernel(tc, image, out):
         def by_run(ap):
             return ap.rearrange("p (o q) -> p o q", q=RUN)
 
-        def square_sides(t):
-            tiles = []
-            for a in range(len(SIDES)):
-                sq = work.tile([P, 2 * UNIT], F32, name="sqr%d" % a, tag="sqr%d" % a, bufs=1)
-                nc.scalar.activation(
-                    out=sq[:].rearrange("c (h j p) -> c h j p", h=2, j=4),
-                    in_=loaded[t][:].rearrange("c (h p j) -> c h j p", h=2, j=4),
-                    func=ACT.Square,
-                    bias=bias_col(SIDES[a]),
-                    scale=1.0,
-                )
-                tiles.append(sq)
-            side_squares[t] = tiles
+        def square_side(t, a):
+            sq = work.tile([P, 2 * UNIT], F32, name="sqr%d" % a, tag="sqr%d" % a, bufs=1)
+            nc.scalar.activation(
+                out=sq[:].rearrange("c (h j p) -> c h j p", h=2, j=4),
+                in_=loaded[t][:].rearrange("c (h p j) -> c h j p", h=2, j=4),
+                func=ACT.Square,
+                bias=bias_col(SIDES[a]),
+                scale=1.0,
+            )
+            side_squares[(t, a)] = sq
 
         def square_mid(t):
             sq = work.tile([P, 2 * UNIT], F32, name="sqm", tag="sqm")
@@ -184,42 +182,44 @@ def tile_colourhistogram_kernel(tc, image, out):
         def line_top(t):
             top_tiles[t].append(top_tile(t, "line", ACT.Identity, col_lin, 2.0 * STEP))
 
-        def add_up(u, k):
+        def add_up(u, i):
             t, h = divmod(u, 2)
+            k = TOP_ORDER[i]
             square, line = top_tiles[t]
             total = ps_e.tile([P, 4, P], F32, name="total", tag="total")
             terms = [square] + k * [line]
             for j in range(4):
                 cols = slice(h * UNIT + j * P, h * UNIT + (j + 1) * P)
-                for i in range(len(terms)):
+                for m in range(len(terms)):
                     nc.tensor.matmul(
                         out=total[:, j, :],
-                        lhsT=terms[i][:, cols],
+                        lhsT=terms[m][:, cols],
                         rhs=ident[:],
-                        start=i == 0,
-                        stop=i == k,
+                        start=m == 0,
+                        stop=m == k,
                         is_transpose=True,
                     )
-            sums[(u, k)] = total
+            sums[(u, i)] = total
 
-        def top_bin(u, k):
+        def top_bin(u, i):
+            k = TOP_ORDER[i]
             nc.scalar.activation(
                 out=bins_of(states[u][3])[:, :, BINS - 1 - k, :].rearrange("p o (g j) -> p o g j", j=4),
-                in_=sums[(u, k)][:].rearrange("p j (o g) -> p o g j", g=4),
+                in_=sums[(u, i)][:].rearrange("p j (o g) -> p o g j", g=4),
                 func=ACT.Exp,
                 bias=bias_col(col_top + k),
                 scale=-INV_2S2,
             )
-            v, k = divmod(u * TOP_BINS + k + 2, TOP_BINS)
+            v, i = divmod(u * TOP_BINS + i + 2, TOP_BINS)
             if v < UNITS:
-                add_up(v, k)
+                add_up(v, i)
 
         def turned_factor(u, a):
             t, h = divmod(u, 2)
             fr = work.tile([P, UNIT], F32, name="fr%d" % a, tag="fr%d" % a)
             nc.scalar.activation(
                 out=fr[:],
-                in_=side_squares[t][a][:, h * UNIT : (h + 1) * UNIT],
+                in_=side_squares[(t, a)][:, h * UNIT : (h + 1) * UNIT],
                 func=ACT.Exp,
                 bias=bias_col(col_shift),
                 scale=-INV_2S2,
@@ -229,9 +229,8 @@ def tile_colourhistogram_kernel(tc, image, out):
                 nc.tensor.transpose(ft[:, j, :], fr[:, j * P : (j + 1) * P], ident[:])
             return ft
 
-        def front(u):
+        def start_unit(u):
             t, h = divmod(u, 2)
-            xu = xts[t][:, h * UNIT : (h + 1) * UNIT]
             fts = [turned_factor(u, 0)]
             if h == 0:
                 both = work.tile([P, 2 * UNIT], F32, name="mid", tag="mid")
@@ -240,21 +239,30 @@ def tile_colourhistogram_kernel(tc, image, out):
                 )
                 mids[t] = both
             gs = work.tile([P, len(OFFSETS), UNIT], F32, name="gs", tag="gs")
-            for i in range(len(OFFSETS)):
+            grp = big.tile([P, OPS * BINS * RUN], BF16, name="grp", tag="grp", align_bytes=64)
+            states[u] = (gs, mids[t][:, h * UNIT : (h + 1) * UNIT], fts, grp)
+
+        def shared_factors(u, lo, hi):
+            t, h = divmod(u, 2)
+            for i in range(lo, hi):
                 r = MAKE_ORDER[i]
                 nc.scalar.activation(
-                    out=gs[:, r, :], in_=xu, func=ACT.Exp, bias=bias_col(col_g + r), scale=slope(OFFSETS[r])
+                    out=states[u][0][:, r, :],
+                    in_=xts[t][:, h * UNIT : (h + 1) * UNIT],
+                    func=ACT.Exp,
+                    bias=bias_col(col_g + r),
+                    scale=slope(OFFSETS[r]),
                 )
-                if u > 0 and i % 2 == 1:
-                    top_bin(u - 1, i // 2)
-            fts.append(turned_factor(u, 1))
-            if u > 0:
-                top_bin(u - 1, TOP_BINS - 1)
-            grp = big.tile([P, OPS * BINS * RUN], BF16, name="grp", tag="grp", align_bytes=64)
-            return (gs, mids[t][:, h * UNIT : (h + 1) * UNIT], fts, grp)
+
+        def second_factor(u):
+            states[u][2].append(turned_factor(u, 1))
 
         def bins_of(grp):
             return grp[:].rearrange("p (o i q) -> p o i q", i=BINS, q=RUN)
+
+        def hold_gpsimd(st):
+            mid = st[1]
+            nc.vector.tensor_scalar_mul(out=mid[:, 0:1], in0=mid[:, 0:1], scalar1=1.0)
 
         def mid_products(st):
             gs, mid, fts, grp = st
@@ -361,7 +369,8 @@ def tile_colourhistogram_kernel(tc, image, out):
             fetch(t)
         turn(0)
         settle(0)
-        square_sides(0)
+        square_side(0, 0)
+        square_side(0, 1)
         square_mid(0)
         square_top(0)
         line_top(0)
@@ -375,15 +384,21 @@ def tile_colourhistogram_kernel(tc, image, out):
                     fetch(t + 3)
                 turn(t + 1)
             if u < UNITS:
-                states[u] = front(u)
-            else:
-                for k in range(TOP_BINS):
-                    top_bin(u - 1, k)
+                start_unit(u)
+                step = 2 + h
+                shared_factors(u, 0, step)
+                top_bin(u, 0)
+                shared_factors(u, step, 2 * step)
+                top_bin(u, 1)
+                shared_factors(u, 2 * step, len(OFFSETS))
+                second_factor(u)
+                top_bin(u, 2)
             if u > 0:
                 cast_sides(states[u - 1])
             if u > 1:
                 multiply(u - 2)
             if u < UNITS:
+                hold_gpsimd(states[u])
                 side_products(states[u])
                 mid_products(states[u])
             if u > 0:
@@ -392,13 +407,19 @@ def tile_colourhistogram_kernel(tc, image, out):
                 pick_diagonal((u - 1) // ROWS_PER_PART - 1)
             if u < UNITS:
                 mid_bin(u, states[u])
-            if ahead and h == 0:
-                settle(t + 1)
-                square_mid(t + 1)
-                square_top(t + 1)
-                line_top(t + 1)
-            if ahead and h == 1:
-                square_sides(t + 1)
+                if ahead and h == 0:
+                    settle(t + 1)
+                top_bin(u, 3)
+                if ahead and h == 0:
+                    square_mid(t + 1)
+                    square_top(t + 1)
+                if ahead and h == 1:
+                    square_side(t + 1, 0)
+                top_bin(u, 4)
+                if ahead and h == 0:
+                    line_top(t + 1)
+                if ahead and h == 1:
+                    square_side(t + 1, 1)
         multiply(UNITS - 1)
         pick_diagonal(IMAGES - 1)
 

@@ -34,7 +34,7 @@ MAKE_ORDER = (3, 2, 1, 0, 4, 5, 6, 7)
 MID = 13
 SIDES = (4, 22)
 UNITS = 64
-CAST_SPLIT = 16
+CAST_SPLIT = 8
 
 
 TOP_ORDER = (0, 4, 1, 3, 2)
@@ -188,15 +188,15 @@ def tile_colourhistogram_kernel(tc, image, out):
             square, line = top_tiles[t]
             total = ps_e.tile([P, 4, P], F32, name="total", tag="total")
             terms = [square] + k * [line]
-            for j in range(4):
-                cols = slice(h * UNIT + j * P, h * UNIT + (j + 1) * P)
-                for m in range(len(terms)):
+            for m in range(len(terms)):
+                for j in range(4):
+                    cols = slice(h * UNIT + j * P, h * UNIT + (j + 1) * P)
                     nc.tensor.matmul(
                         out=total[:, j, :],
                         lhsT=terms[m][:, cols],
                         rhs=ident[:],
-                        start=m == 0,
-                        stop=m == k,
+                        start=m + j == 0,
+                        stop=m == k and j == 3,
                         is_transpose=True,
                     )
             sums[(u, i)] = total
@@ -229,18 +229,22 @@ def tile_colourhistogram_kernel(tc, image, out):
                 nc.tensor.transpose(ft[:, j, :], fr[:, j * P : (j + 1) * P], ident[:])
             return ft
 
-        def start_unit(u):
+        def mid_factor(t):
+            both = work.tile([P, 2 * UNIT], F32, name="mid", tag="mid")
+            nc.scalar.activation(
+                out=both[:], in_=mid_squares[t][:], func=ACT.Exp, bias=bias_col(col_mid), scale=-INV_2S2
+            )
+            mids[t] = both
+
+        def mid_of(u):
             t, h = divmod(u, 2)
+            return mids[t][:, h * UNIT : (h + 1) * UNIT]
+
+        def start_unit(u):
             fts = [turned_factor(u, 0)]
-            if h == 0:
-                both = work.tile([P, 2 * UNIT], F32, name="mid", tag="mid")
-                nc.scalar.activation(
-                    out=both[:], in_=mid_squares[t][:], func=ACT.Exp, bias=bias_col(col_mid), scale=-INV_2S2
-                )
-                mids[t] = both
             gs = work.tile([P, len(OFFSETS), UNIT], F32, name="gs", tag="gs")
             grp = big.tile([P, OPS * BINS * RUN], BF16, name="grp", tag="grp", align_bytes=64)
-            states[u] = (gs, mids[t][:, h * UNIT : (h + 1) * UNIT], fts, grp)
+            states[u] = (gs, mid_of(u), fts, grp)
 
         def shared_factors(u, lo, hi):
             t, h = divmod(u, 2)
@@ -260,9 +264,9 @@ def tile_colourhistogram_kernel(tc, image, out):
         def bins_of(grp):
             return grp[:].rearrange("p (o i q) -> p o i q", i=BINS, q=RUN)
 
-        def hold_gpsimd(st):
-            mid = st[1]
-            nc.vector.tensor_scalar_mul(out=mid[:, 0:1], in0=mid[:, 0:1], scalar1=1.0)
+        def hold_gpsimd(u):
+            column = mid_of(u)[:, 0:1]
+            nc.vector.tensor_scalar_mul(out=column, in0=column, scalar1=1.0)
 
         def mid_products(st):
             gs, mid, fts, grp = st
@@ -318,11 +322,13 @@ def tile_colourhistogram_kernel(tc, image, out):
                     scale=pow(EULER, -SHIFT),
                 )
 
-        def quantise(st):
-            grp = st[3]
+        def quantise(u):
+            grp = states[u][3]
             codes = mxp.tile([P, OPS * P], U32, name="codes", tag="codes", align_bytes=64)
             plane = mxp.tile([P, OPS * P], U8, name="plane", tag="plane", align_bytes=64)
             for q in range(4):
+                if q == 3 and u + 2 < UNITS:
+                    hold_gpsimd(u + 2)
                 nc.vector.quantize_mx(
                     out=codes[:, q * 1024 : (q + 1) * 1024].bitcast(FP8X4),
                     scales=plane[:, q * 1024 : (q + 1) * 1024],
@@ -374,6 +380,7 @@ def tile_colourhistogram_kernel(tc, image, out):
         square_mid(0)
         square_top(0)
         line_top(0)
+        mid_factor(0)
         add_up(0, 0)
         add_up(0, 1)
         for u in range(UNITS + 1):
@@ -393,16 +400,17 @@ def tile_colourhistogram_kernel(tc, image, out):
                 shared_factors(u, 2 * step, len(OFFSETS))
                 second_factor(u)
                 top_bin(u, 2)
+                if ahead and h == 1:
+                    mid_factor(t + 1)
             if u > 0:
                 cast_sides(states[u - 1])
             if u > 1:
                 multiply(u - 2)
             if u < UNITS:
-                hold_gpsimd(states[u])
                 side_products(states[u])
                 mid_products(states[u])
             if u > 0:
-                quants[u - 1] = quantise(states[u - 1])
+                quants[u - 1] = quantise(u - 1)
             if u > 1 and (u - 1) % ROWS_PER_PART == 0:
                 pick_diagonal((u - 1) // ROWS_PER_PART - 1)
             if u < UNITS:

from contextlib import ExitStack

import concourse.mybir as mybir
from concourse.masks import make_identity

F32 = mybir.dt.float32
BF16 = mybir.dt.bfloat16
U32 = mybir.dt.uint32
U8 = mybir.dt.uint8
FP8X4 = mybir.dt.float8_e4m3fn_x4
ACT = mybir.ActivationFunctionType
ALU = mybir.AluOpType
AX = mybir.AxisListType

P = 128
IMAGES = 8
BINS = 32
ROWS_PER_PART = 8
ROW = 512
UNIT = 512
OPS = 32
RUN = 16

FLOPS = 2 * IMAGES * 512 * 512 * BINS * BINS

EULER = 2.718281828459045
INV_2S2 = 200.0
STEP = 1.0 / 31.0
SHIFT = 45.0
SHIFT_MID = 39.5

OFFSETS = (-4, -3, -2, -1, 1, 2, 3, 4)
MAKE_ORDER = (3, 2, 1, 0, 4, 5, 6, 7)
MID = 13
SIDES = (4, 22)
UNITS = 64
CAST_SPLIT = 8


TOP_ORDER = (0, 4, 1, 3, 2)
TOP_BINS = 5


def slope(r):
    return 2.0 * INV_2S2 * r * STEP


def tile_colourhistogram_kernel(tc, image, out):
    nc = tc.nc
    with ExitStack() as ctx:
        const = ctx.enter_context(tc.tile_pool(name="const", bufs=1))
        load = ctx.enter_context(tc.tile_pool(name="load", bufs=4))
        xpool = ctx.enter_context(tc.tile_pool(name="xpool", bufs=2))
        work = ctx.enter_context(tc.tile_pool(name="work", bufs=2))
        big = ctx.enter_context(tc.tile_pool(name="big", bufs=3))
        mxp = ctx.enter_context(tc.tile_pool(name="mxp", bufs=2))
        ps_x = ctx.enter_context(tc.psum_pool(name="ps_x", bufs=1))
        ps_e = ctx.enter_context(tc.psum_pool(name="ps_e", bufs=2))
        ps_p = ctx.enter_context(tc.psum_pool(name="ps_p", bufs=2))
        ps_acc = ctx.enter_context(tc.psum_pool(name="ps_acc", bufs=1))

        col_g = BINS
        col_shift = BINS + len(OFFSETS)
        col_mid = col_shift + 1
        col_top = col_mid + 1
        col_lin = col_top + TOP_BINS
        biases = const.tile([P, col_lin + 1], F32, name="biases")
        for k in range(TOP_BINS):
            nc.vector.memset(biases[:, col_top + k : col_top + k + 1], float(200 * k * k))
        nc.vector.memset(biases[:, col_lin : col_lin + 1], 1.0)
        nc.vector.tensor_scalar_mul(
            out=biases[:, col_top:col_lin], in0=biases[:, col_top:col_lin], scalar1=-STEP * STEP
        )
        nc.vector.tensor_scalar_mul(
            out=biases[:, col_lin : col_lin + 1], in0=biases[:, col_lin : col_lin + 1], scalar1=-2.0 * STEP
        )
        for i in range(BINS):
            nc.vector.memset(biases[:, i : i + 1], float(i))
        for t in range(len(OFFSETS)):
            r = OFFSETS[t]
            nc.vector.memset(biases[:, col_g + t : col_g + t + 1], float(400 * r * MID + 200 * r * r))
        nc.vector.memset(biases[:, col_shift : col_shift + 1], SHIFT)
        nc.vector.memset(biases[:, col_mid : col_mid + 1], SHIFT_MID)
        nc.vector.tensor_scalar_mul(out=biases[:, 0:BINS], in0=biases[:, 0:BINS], scalar1=-STEP)
        nc.vector.tensor_scalar(
            out=biases[:, col_g:col_shift],
            in0=biases[:, col_g:col_shift],
            scalar1=-STEP * STEP,
            scalar2=-SHIFT_MID,
            op0=ALU.mult,
            op1=ALU.add,
        )

        ident = const.tile([P, P], F32, name="ident")
        make_identity(nc, ident[:])
        same_g = const.tile([P, 4], F32, name="same_g")
        nc.vector.tensor_reduce(
            out=same_g[:], in_=ident[:].rearrange("p (i g) -> p g i", g=4), axis=AX.X, op=ALU.add
        )
        fold = const.tile([P, P], F32, name="fold")
        nc.vector.memset(fold[:], 0.0)
        nc.vector.tensor_reduce(
            out=fold[:, 0:BINS], in_=ident[:].rearrange("p (i g) -> p i g", g=4), axis=AX.X, op=ALU.add
        )
        diag = const.tile([P, IMAGES * BINS], F32, name="diag")

        loaded = {}
        xts = {}
        accs = {}

        turned_x = {}
        side_squares = {}
        mid_squares = {}
        top_tiles = {}
        sums = {}
        states = {}
        quants = {}
        mids = {}

        def fetch(t):
            n, pair = divmod(t, ROWS_PER_PART // 2)
            loaded[t] = load.tile([P, 2 * ROW], BF16, name="raw", tag="raw")
            rows = image[n].rearrange("h (c k) w -> (h c) k w", k=ROWS_PER_PART)
            nc.sync.dma_start(
                out=loaded[t][:].rearrange("c (h x) -> c h x", h=2),
                in_=rows[:, 2 * pair : 2 * pair + 2],
            )

        def turn(t):
            words = loaded[t][:].bitcast(F32)
            xp = ps_x.tile([P, 2, 2, P], F32, name="xp", tag="xp")
            for h in range(2):
                for e in range(2):
                    base = h * 256
                    nc.tensor.transpose(xp[:, h, e, :], words[:, base + e : base + 256 : 2], ident[:])
            turned_x[t] = xp

        def settle(t):
            xt = xpool.tile([P, 2 * UNIT], BF16, name="xt", tag="xt")
            nc.scalar.copy(
                out=xt[:].bitcast(F32).rearrange("p (h c e) -> p h c e", h=2, e=2),
                in_=turned_x[t][:].rearrange("p h e c -> p h c e"),
            )
            xts[t] = xt

        def bias_col(c):
            return biases[:, c : c + 1]

        def by_run(ap):
            return ap.rearrange("p (o q) -> p o q", q=RUN)

        def square_side(t, a):
            sq = work.tile([P, 2 * UNIT], F32, name="sqr%d" % a, tag="sqr%d" % a, bufs=1)
            nc.scalar.activation(
                out=sq[:].rearrange("c (h j p) -> c h j p", h=2, j=4),
                in_=loaded[t][:].rearrange("c (h p j) -> c h j p", h=2, j=4),
                func=ACT.Square,
                bias=bias_col(SIDES[a]),
                scale=1.0,
            )
            side_squares[(t, a)] = sq

        def square_mid(t):
            sq = work.tile([P, 2 * UNIT], F32, name="sqm", tag="sqm")
            nc.scalar.activation(out=sq[:], in_=xts[t][:], func=ACT.Square, bias=bias_col(MID), scale=1.0)
            mid_squares[t] = sq

        def top_tile(t, name, func, col, scale):
            tile = work.tile([P, 2 * UNIT], F32, name=name, tag=name)
            nc.scalar.activation(
                out=tile[:].rearrange("c (h j p) -> c h j p", h=2, j=4),
                in_=loaded[t][:].rearrange("c (h p j) -> c h j p", h=2, j=4),
                func=func,
                bias=bias_col(col),
                scale=scale,
            )
            return tile

        def square_top(t):
            top_tiles[t] = [top_tile(t, "top", ACT.Square, BINS - 1, 1.0)]

        def line_top(t):
            top_tiles[t].append(top_tile(t, "line", ACT.Identity, col_lin, 2.0 * STEP))

        def add_up(u, i):
            t, h = divmod(u, 2)
            k = TOP_ORDER[i]
            square, line = top_tiles[t]
            total = ps_e.tile([P, 4, P], F32, name="total", tag="total")
            terms = [square] + k * [line]
            for m in range(len(terms)):
                for j in range(4):
                    cols = slice(h * UNIT + j * P, h * UNIT + (j + 1) * P)
                    nc.tensor.matmul(
                        out=total[:, j, :],
                        lhsT=terms[m][:, cols],
                        rhs=ident[:],
                        start=m + j == 0,
                        stop=m == k and j == 3,
                        is_transpose=True,
                    )
            sums[(u, i)] = total

        def top_bin(u, i):
            k = TOP_ORDER[i]
            nc.scalar.activation(
                out=bins_of(states[u][3])[:, :, BINS - 1 - k, :].rearrange("p o (g j) -> p o g j", j=4),
                in_=sums[(u, i)][:].rearrange("p j (o g) -> p o g j", g=4),
                func=ACT.Exp,
                bias=bias_col(col_top + k),
                scale=-INV_2S2,
            )
            v, i = divmod(u * TOP_BINS + i + 2, TOP_BINS)
            if v < UNITS:
                add_up(v, i)

        def turned_factor(u, a):
            t, h = divmod(u, 2)
            fr = work.tile([P, UNIT], F32, name="fr%d" % a, tag="fr%d" % a)
            nc.scalar.activation(
                out=fr[:],
                in_=side_squares[(t, a)][:, h * UNIT : (h + 1) * UNIT],
                func=ACT.Exp,
                bias=bias_col(col_shift),
                scale=-INV_2S2,
            )
            ft = ps_p.tile([P, 4, P], F32, name="ft%d" % a, tag="ft%d" % a)
            for j in range(4):
                nc.tensor.transpose(ft[:, j, :], fr[:, j * P : (j + 1) * P], ident[:])
            return ft

        def mid_factor(t):
            both = work.tile([P, 2 * UNIT], F32, name="mid", tag="mid")
            nc.scalar.activation(
                out=both[:], in_=mid_squares[t][:], func=ACT.Exp, bias=bias_col(col_mid), scale=-INV_2S2
            )
            mids[t] = both

        def mid_of(u):
            t, h = divmod(u, 2)
            return mids[t][:, h * UNIT : (h + 1) * UNIT]

        def start_unit(u):
            fts = [turned_factor(u, 0)]
            gs = work.tile([P, len(OFFSETS), UNIT], F32, name="gs", tag="gs")
            grp = big.tile([P, OPS * BINS * RUN], BF16, name="grp", tag="grp", align_bytes=64)
            states[u] = (gs, mid_of(u), fts, grp)

        def shared_factors(u, lo, hi):
            t, h = divmod(u, 2)
            for i in range(lo, hi):
                r = MAKE_ORDER[i]
                nc.scalar.activation(
                    out=states[u][0][:, r, :],
                    in_=xts[t][:, h * UNIT : (h + 1) * UNIT],
                    func=ACT.Exp,
                    bias=bias_col(col_g + r),
                    scale=slope(OFFSETS[r]),
                )

        def second_factor(u):
            states[u][2].append(turned_factor(u, 1))

        def bins_of(grp):
            return grp[:].rearrange("p (o i q) -> p o i q", i=BINS, q=RUN)

        def hold_gpsimd(u):
            column = mid_of(u)[:, 0:1]
            nc.vector.tensor_scalar_mul(out=column, in0=column, scalar1=1.0)

        def mid_products(st):
            gs, mid, fts, grp = st
            g4 = bins_of(grp)
            for half in range(2):
                lo = MID - 4 + 5 * half
                nc.gpsimd.tensor_tensor(
                    out=g4[:, :, lo : lo + 4, :].rearrange("p o i q -> p i o q"),
                    in0=gs[:, 4 * half : 4 * half + 4, :].rearrange("p i (o q) -> p i o q", q=RUN),
                    in1=by_run(mid).unsqueeze(1).to_broadcast([P, 4, OPS, RUN]),
                    op=ALU.mult,
                )

        def side_products(st):
            gs, mid, fts, grp = st
            g4 = bins_of(grp)
            for a in range(len(SIDES)):
                m = SIDES[a]
                turned = fts[a][:].rearrange("p j (o g) -> p o g j", g=4)
                for t in MAKE_ORDER:
                    r = OFFSETS[t]
                    nc.vector.scalar_tensor_tensor(
                        out=g4[:, :, m + r, :].rearrange("p o (g j) -> p o g j", j=4),
                        in0=gs[:, t, :].rearrange("p (o g j) -> p o g j", g=4, j=4),
                        scalar=pow(EULER, SHIFT_MID - SHIFT + slope(r) * (MID - m) * STEP),
                        in1=turned,
                        op0=ALU.mult,
                        op1=ALU.mult,
                    )
                if a == 1:
                    nc.vector.tensor_scalar_mul(
                        out=g4[:, 0:CAST_SPLIT, m, :].rearrange("p o (g j) -> p o g j", j=4),
                        in0=turned[:, 0:CAST_SPLIT],
                        scalar1=pow(EULER, -SHIFT),
                    )

        def mid_bin(u, st):
            t, h = divmod(u, 2)
            nc.scalar.activation(
                out=bins_of(st[3])[:, :, MID, :],
                in_=by_run(mid_squares[t][:, h * UNIT : (h + 1) * UNIT]),
                func=ACT.Exp,
                scale=-INV_2S2,
            )

        def cast_sides(st):
            gs, mid, fts, grp = st
            for a, lo in ((0, 0), (1, CAST_SPLIT)):
                nc.scalar.activation(
                    out=bins_of(grp)[:, lo:OPS, SIDES[a], :].rearrange("p o (g j) -> p o g j", j=4),
                    in_=fts[a][:].rearrange("p j (o g) -> p o g j", g=4)[:, lo:OPS],
                    func=ACT.Copy,
                    scale=pow(EULER, -SHIFT),
                )

        def quantise(u):
            grp = states[u][3]
            codes = mxp.tile([P, OPS * P], U32, name="codes", tag="codes", align_bytes=64)
            plane = mxp.tile([P, OPS * P], U8, name="plane", tag="plane", align_bytes=64)
            for q in range(4):
                if q == 3 and u + 2 < UNITS:
                    hold_gpsimd(u + 2)
                nc.vector.quantize_mx(
                    out=codes[:, q * 1024 : (q + 1) * 1024].bitcast(FP8X4),
                    scales=plane[:, q * 1024 : (q + 1) * 1024],
                    in_=grp[:, q * 4096 : (q + 1) * 4096],
                )
            return (codes, plane)

        def multiply(u):
            n, k = divmod(u, ROWS_PER_PART)
            if k == 0:
                accs[n] = ps_acc.tile([P, P], F32, name="acc", tag="acc")
            codes, plane = quants[u]
            half = OPS // 2
            for o in range(half):
                a = slice(o * P, (o + 1) * P)
                b = slice((half + o) * P, (half + o + 1) * P)
                nc.tensor.matmul_mx(
                    out=accs[n][:],
                    lhsT=codes[:, a].bitcast(FP8X4),
                    lhsT_scale=plane[:, a],
                    rhs=codes[:, b].bitcast(FP8X4),
                    rhs_scale=plane[:, b],
                    start=(k == 0 and o == 0),
                    stop=(k == ROWS_PER_PART - 1 and o == half - 1),
                )

        def pick_diagonal(n):
            kept = work.tile([P, P], F32, name="kept", tag="kept")
            nc.vector.tensor_tensor(
                out=kept[:].rearrange("p (j g) -> p j g", g=4),
                in0=accs[n][:].rearrange("p (j g) -> p j g", g=4),
                in1=same_g[:].unsqueeze(1).to_broadcast([P, BINS, 4]),
                op=ALU.mult,
            )
            nc.vector.tensor_reduce(
                out=diag[:, n * BINS : (n + 1) * BINS],
                in_=kept[:].rearrange("p (j g) -> p j g", g=4),
                axis=AX.X,
                op=ALU.add,
            )

        ctx.enter_context(tc.manual_schedule())
        for t in range(3):
            fetch(t)
        turn(0)
        settle(0)
        square_side(0, 0)
        square_side(0, 1)
        square_mid(0)
        square_top(0)
        line_top(0)
        mid_factor(0)
        add_up(0, 0)
        add_up(0, 1)
        for u in range(UNITS + 1):
            t, h = divmod(u, 2)
            ahead = u < UNITS and t + 1 < UNITS // 2
            if ahead and h == 0:
                if t + 3 < UNITS // 2:
                    fetch(t + 3)
                turn(t + 1)
            if u < UNITS:
                start_unit(u)
                step = 2 + h
                shared_factors(u, 0, step)
                top_bin(u, 0)
                shared_factors(u, step, 2 * step)
                top_bin(u, 1)
                shared_factors(u, 2 * step, len(OFFSETS))
                second_factor(u)
                top_bin(u, 2)
                if ahead and h == 1:
                    mid_factor(t + 1)
            if u > 0:
                cast_sides(states[u - 1])
            if u > 1:
                multiply(u - 2)
            if u < UNITS:
                side_products(states[u])
                mid_products(states[u])
            if u > 0:
                quants[u - 1] = quantise(u - 1)
            if u > 1 and (u - 1) % ROWS_PER_PART == 0:
                pick_diagonal((u - 1) // ROWS_PER_PART - 1)
            if u < UNITS:
                mid_bin(u, states[u])
                if ahead and h == 0:
                    settle(t + 1)
                top_bin(u, 3)
                if ahead and h == 0:
                    square_mid(t + 1)
                    square_top(t + 1)
                if ahead and h == 1:
                    square_side(t + 1, 0)
                top_bin(u, 4)
                if ahead and h == 0:
                    line_top(t + 1)
                if ahead and h == 1:
                    square_side(t + 1, 1)
        multiply(UNITS - 1)
        pick_diagonal(IMAGES - 1)

        fin = ps_x.tile([P, IMAGES * BINS], F32, name="fin", tag="xp")
        nc.tensor.matmul(out=fin[:], lhsT=fold[:], rhs=diag[:], start=True, stop=True)
        res = const.tile([P, IMAGES * BINS], F32, name="res")
        nc.vector.tensor_copy(out=res[:], in_=fin[:])
        nc.sync.dma_start(
            out=out.rearrange("n o i j -> i (n o) j"),
            in_=res[0:BINS, :].rearrange("i (n j) -> i n j", j=BINS),
        )
